import numpy as np
import ml_dtypes


def mxq(x, axis, fmt="e4m3"):
    dtype, down = {"e4m3": (ml_dtypes.float8_e4m3fn, 7), "e5m2": (ml_dtypes.float8_e5m2, 14)}[fmt]
    v = np.moveaxis(np.asarray(x, np.float32).astype(ml_dtypes.bfloat16).astype(np.float64), axis, -1)
    blocks = v.reshape(v.shape[:-1] + (-1, 32))
    amax = np.abs(blocks).max(-1, keepdims=True)
    byte = np.maximum(np.where(amax > 0, np.frexp(amax)[1] - 1 + 127, 0) - down, 1)
    scale = np.exp2(byte - 127.0)
    codes = (blocks / scale).astype(np.float32).astype(dtype).astype(np.float64)
    return np.moveaxis((codes * scale).reshape(v.shape), -1, axis)


WIDE = False


def mx_kscale(k):
    if not WIDE:
        return np.ones(k)
    levels = np.array([10, -10, 5, -5, 0])
    a = np.random.permutation(np.resize(levels, k // 512 * 4)).reshape(k // 512, 4)
    idx = np.arange(k)
    return np.exp2(a[idx // 512, idx % 128 // 32])


BF16 = ml_dtypes.bfloat16


def bf(x):
    return np.asarray(x, np.float32).astype(BF16)


def f64(x):
    return np.asarray(x).astype(np.float64)


B, C, H, W, F = 4, 512, 64, 64, 256


def setup_inputs():
    t = np.exp2(np.round(np.log2(mx_kscale(C)) / 2))
    return {"inputs": bf(np.random.standard_normal((B, C, H, W)) * 2.0 + 2.0 * np.log(t)[None, :, None, None]),
            "biases": bf(np.random.standard_normal((1, 1, C, F)) / t[:, None])}


def _mix_weights(biases):
    sq = biases * biases
    p = sq / np.sum(sq, axis=2, keepdims=True)
    return p.reshape(C, F)


def reference(inputs, biases):
    x = f64(inputs)
    p = _mix_weights(f64(biases))
    m = np.max(x, axis=1, keepdims=True)
    e = np.exp(x - m)
    eq = mxq(e, 1, "e4m3")
    pq = mxq(p, 0, "e4m3")
    s = np.matmul(pq.T, eq.reshape(B, C, H * W)).reshape(B, F, H, W)
    return m + np.log(s)

@@ -1,0 +1,189 @@
+from contextlib import ExitStack
+
+import concourse.mybir as mybir
+from concourse.masks import make_identity
+
+BF16 = mybir.dt.bfloat16
+F32 = mybir.dt.float32
+U32 = mybir.dt.uint32
+U8 = mybir.dt.uint8
+FP8X4 = mybir.dt.float8_e4m3fn_x4
+ALU = mybir.AluOpType
+ACT = mybir.ActivationFunctionType
+AX = mybir.AxisListType
+
+P = 128
+B, C, HW, F = 4, 512, 4096, 256
+J = 4
+BLK = 1024
+NB = B * HW // BLK
+SUB = BLK // P
+GS = 3
+GW = GS * P
+VW = BLK - GW
+FLOPS = 2 * B * HW * C * F
+
+
+def tile_mixture_t_kernel(tc, inputs, biases, out):
+    nc = tc.nc
+    x = inputs.rearrange("b (p j) h w -> b p j (h w)", j=J)
+    bia = biases[0, 0].rearrange("(p j) f -> p j f", j=J)
+    o = out.rearrange("b (t f) h w -> b t f (h w)", t=2)
+
+    with ExitStack() as ctx:
+        ctx.enter_context(tc.manual_schedule())
+        keep = ctx.enter_context(tc.tile_pool(name="keep", bufs=1))
+        ps_x = ctx.enter_context(tc.psum_pool(name="ps_x", bufs=2))
+        ps_v = ctx.enter_context(tc.psum_pool(name="ps_v", bufs=2))
+        ps_g = ctx.enter_context(tc.psum_pool(name="ps_g", bufs=1))
+        ps_s = ctx.enter_context(tc.psum_pool(name="ps_s", bufs=3))
+
+        ident = keep.tile([P, P], BF16)
+        ones = keep.tile([P, P], F32)
+        codes = keep.tile([P, B * HW], U32, align_bytes=64)
+        scales = keep.tile([P, B * HW], U8, align_bytes=64)
+        m_t = keep.tile([P, NB * SUB], BF16)
+        mbs = keep.tile([P, NB, GW], BF16)
+        b_raw = keep.tile([P, J, F], BF16)
+        sq = keep.tile([P, J, F], F32)
+        js1 = keep.tile([P, 2, F], F32)
+        js = keep.tile([P, F], F32)
+        rs = keep.tile([P, F], F32)
+        p_grp = keep.tile([P, F, J], BF16, align_bytes=64)
+        p_codes = keep.tile([P, F], U32, align_bytes=64)
+        p_scales = keep.tile([P, F], U8, align_bytes=64)
+
+        nc.sync.dma_start(out=b_raw[:], in_=bia)
+        make_identity(nc, ident[:])
+        nc.gpsimd.memset(ones[:], 1.0)
+
+        def bcast(k, first, mb_v, mb_g):
+            for i in range(first, SUB):
+                dst = mb_g if i < GS else mb_v
+                nc.tensor.transpose(
+                    dst[:, i * P : (i + 1) * P],
+                    m_t[:, k * SUB + i : k * SUB + i + 1].to_broadcast([P, P]),
+                    ident[:],
+                )
+
+        with ExitStack() as ph1:
+            t_pool = ph1.enter_context(tc.tile_pool(name="t_pool", bufs=4))
+            w_pool = ph1.enter_context(tc.tile_pool(name="w_pool", bufs=2))
+            d_pool = ph1.enter_context(tc.tile_pool(name="d_pool", bufs=2))
+            g_pool = ph1.enter_context(tc.tile_pool(name="g_pool", bufs=3))
+            t_of, xmt_of, mbv_of, dg_of, grp_of = {}, {}, {}, {}, {}
+
+            def load(k):
+                t_in = t_pool.tile([P, J, BLK], BF16)
+                px = (k % 4) * BLK
+                nc.sync.dma_start(out=t_in[:], in_=x[k // 4, :, :, px : px + BLK])
+                t_of[k] = t_in
+
+            load(0)
+            load(1)
+            nc.scalar.activation(out=sq[:], in_=b_raw[:], func=ACT.Square)
+            nc.gpsimd.tensor_tensor(out=js1[:], in0=sq[:, 0:2, :], in1=sq[:, 2:4, :], op=ALU.add)
+            nc.gpsimd.tensor_tensor(out=js[:], in0=js1[:, 0, :], in1=js1[:, 1, :], op=ALU.add)
+
+            for it in range(NB + 3):
+                if it < NB:
+                    t_in = t_of[it]
+                    a2 = w_pool.tile([P, 2, BLK], BF16)
+                    xm = w_pool.tile([P, BLK], BF16)
+                    nc.vector.tensor_tensor(out=a2[:], in0=t_in[:, 0:2, :], in1=t_in[:, 2:4, :], op=ALU.max)
+                    nc.vector.tensor_tensor(out=xm[:], in0=a2[:, 0, :], in1=a2[:, 1, :], op=ALU.max)
+                    xmt = ps_x.tile([P, SUB, P], BF16)
+                    for i in range(SUB):
+                        nc.tensor.transpose(xmt[:, i, :], xm[:, i * P : (i + 1) * P], ident[:])
+                    xmt_of[it] = xmt
+                if it == 0:
+                    col_sum = ps_s.tile([P, 512], F32, tag="s")
+                    nc.tensor.matmul(out=col_sum[:, 0:F], lhsT=ones[:], rhs=js[:], start=True, stop=True)
+                k = it - 1
+                if 0 <= k < NB:
+                    with nc.allow_low_precision(reason="a maximum of bfloat16 values is a bfloat16 value"):
+                        nc.vector.tensor_reduce(
+                            out=m_t[:, k * SUB : (k + 1) * SUB], in_=xmt_of[k][:], axis=AX.X, op=ALU.max
+                        )
+                    mb_v = ps_v.tile([P, BLK], BF16)
+                    mb_g = ps_g.tile([P, BLK], BF16)
+                    bcast(k, 0, mb_v, mb_g)
+                    mbv_of[k] = mb_v
+                k2 = it - 2
+                if 0 <= k2 < NB:
+                    grp = g_pool.tile([P, BLK * J], BF16, align_bytes=64)
+                    grp_of[k2] = grp
+                    nc.scalar.activation(
+                        out=grp[:, 0 : GW * J], in_=dg_of[k2][:].rearrange("p w j -> p (w j)"), func=ACT.Exp
+                    )
+                if 0 <= k < NB:
+                    nc.scalar.copy(out=mbs[:, k, :], in_=mb_g[:, 0:GW])
+                    d_g = d_pool.tile([P, GW, J], F32)
+                    nc.gpsimd.tensor_tensor(
+                        out=d_g[:],
+                        in0=t_of[k][:, :, 0:GW].rearrange("p j w -> p w j"),
+                        in1=mbs[:, k, :].unsqueeze(2).to_broadcast([P, GW, J]),
+                        op=ALU.subtract,
+                    )
+                    dg_of[k] = d_g
+                if 0 <= k2 < NB:
+                    d_v = d_pool.tile([P, VW, J], F32)
+                    nc.vector.tensor_tensor(
+                        out=d_v[:],
+                        in0=t_of[k2][:, :, GW:BLK].rearrange("p j w -> p w j"),
+                        in1=mbv_of[k2][:, GW:BLK].unsqueeze(2).to_broadcast([P, VW, J]),
+                        op=ALU.subtract,
+                    )
+                    nc.scalar.activation(
+                        out=grp_of[k2][:, GW * J : BLK * J], in_=d_v[:].rearrange("p w j -> p (w j)"), func=ACT.Exp
+                    )
+                if it + 2 < NB:
+                    load(it + 2)
+                k3 = it - 3
+                if 0 <= k3 < NB:
+                    nc.vector.quantize_mx(
+                        out=codes[:, k3 * BLK : (k3 + 1) * BLK].bitcast(FP8X4),
+                        scales=scales[:, k3 * BLK : (k3 + 1) * BLK],
+                        in_=grp_of[k3][:],
+                    )
+                if it == 1:
+                    nc.vector.reciprocal(out=rs[:], in_=col_sum[:, 0:F])
+                    nc.gpsimd.tensor_tensor(
+                        out=p_grp[:],
+                        in0=sq[:].rearrange("p j f -> p f j"),
+                        in1=rs[:].unsqueeze(2).to_broadcast([P, F, J]),
+                        op=ALU.mult,
+                    )
+                if it == 2:
+                    nc.vector.quantize_mx(
+                        out=p_codes[:].bitcast(FP8X4),
+                        scales=p_scales[:],
+                        in_=p_grp[:].rearrange("p f j -> p (f j)"),
+                    )
+
+        with ExitStack() as ph2:
+            o_pool = ph2.enter_context(tc.tile_pool(name="o_pool", bufs=3))
+            for k in range(NB):
+                mb_v = ps_v.tile([P, BLK], BF16)
+                bcast(k, GS, mb_v, mb_v)
+                px = (k % 4) * BLK
+                for ft in range(2):
+                    o_t = o_pool.tile([P, BLK], F32, tag="o%d" % ft)
+                    for h in range(2):
+                        cols = slice(k * BLK + h * 512, k * BLK + (h + 1) * 512)
+                        s = ps_s.tile([P, 512], F32, tag="s")
+                        nc.tensor.matmul_mx(
+                            out=s[:],
+                            lhsT=p_codes[:, ft * P : (ft + 1) * P].bitcast(FP8X4),
+                            lhsT_scale=p_scales[:, ft * P : (ft + 1) * P],
+                            rhs=codes[:, cols].bitcast(FP8X4),
+                            rhs_scale=scales[:, cols],
+                            start=True,
+                            stop=True,
+                        )
+                        nc.scalar.activation(out=o_t[:, h * 512 : (h + 1) * 512], in_=s[:], func=ACT.Ln)
+                    nc.gpsimd.tensor_tensor(out=o_t[:, 0:GW], in0=o_t[:, 0:GW], in1=mbs[:, k, :], op=ALU.add)
+                    nc.vector.tensor_tensor(
+                        out=o_t[:, GW:BLK], in0=o_t[:, GW:BLK], in1=mb_v[:, GW:BLK], op=ALU.add
+                    )
+                    nc.sync.dma_start(out=o[k // 4, ft, :, px : px + BLK], in_=o_t[:])

@@ -119,12 +119,13 @@ def tile_mixture_t_kernel(tc, inputs, biases, out):
                 if 0 <= k < NB:
                     nc.scalar.copy(out=mbs[:, k, :], in_=mb_g[:, 0:GW])
                     d_g = d_pool.tile([P, GW, J], F32)
-                    nc.gpsimd.tensor_tensor(
-                        out=d_g[:],
-                        in0=t_of[k][:, :, 0:GW].rearrange("p j w -> p w j"),
-                        in1=mbs[:, k, :].unsqueeze(2).to_broadcast([P, GW, J]),
-                        op=ALU.subtract,
-                    )
+                    for i in range(GS):
+                        nc.gpsimd.tensor_tensor(
+                            out=d_g[:, i * P : (i + 1) * P, :],
+                            in0=t_of[k][:, :, i * P : (i + 1) * P].rearrange("p j w -> p w j"),
+                            in1=mbs[:, k, i * P : (i + 1) * P].unsqueeze(2).to_broadcast([P, P, J]),
+                            op=ALU.subtract,
+                        )
                     dg_of[k] = d_g
                 if 0 <= k2 < NB:
                     d_v = d_pool.tile([P, VW, J], F32)

@@ -18,9 +18,9 @@ J = 4
 BLK = 1024
 NB = B * HW // BLK
 SUB = BLK // P
-GS = 3
-GW = GS * P
-VW = BLK - GW
+NBG = 4
+BW = NBG * P
+AW = BLK - BW
 FLOPS = 2 * B * HW * C * F
 
 
@@ -33,17 +33,14 @@ def tile_mixture_t_kernel(tc, inputs, biases, out):
     with ExitStack() as ctx:
         ctx.enter_context(tc.manual_schedule())
         keep = ctx.enter_context(tc.tile_pool(name="keep", bufs=1))
-        ps_x = ctx.enter_context(tc.psum_pool(name="ps_x", bufs=2))
         ps_v = ctx.enter_context(tc.psum_pool(name="ps_v", bufs=2))
-        ps_g = ctx.enter_context(tc.psum_pool(name="ps_g", bufs=1))
-        ps_s = ctx.enter_context(tc.psum_pool(name="ps_s", bufs=3))
 
         ident = keep.tile([P, P], BF16)
         ones = keep.tile([P, P], F32)
         codes = keep.tile([P, B * HW], U32, align_bytes=64)
         scales = keep.tile([P, B * HW], U8, align_bytes=64)
         m_t = keep.tile([P, NB * SUB], BF16)
-        mbs = keep.tile([P, NB, GW], BF16)
+        neg_m = keep.tile([P, NB, NBG], F32)
         b_raw = keep.tile([P, J, F], BF16)
         sq = keep.tile([P, J, F], F32)
         js1 = keep.tile([P, 2, F], F32)
@@ -57,21 +54,23 @@ def tile_mixture_t_kernel(tc, inputs, biases, out):
         make_identity(nc, ident[:])
         nc.gpsimd.memset(ones[:], 1.0)
 
-        def bcast(k, first, mb_v, mb_g):
+        def bcast(k, first, mb_v):
             for i in range(first, SUB):
-                dst = mb_g if i < GS else mb_v
                 nc.tensor.transpose(
-                    dst[:, i * P : (i + 1) * P],
+                    mb_v[:, i * P : (i + 1) * P],
                     m_t[:, k * SUB + i : k * SUB + i + 1].to_broadcast([P, P]),
                     ident[:],
                 )
 
         with ExitStack() as ph1:
+            ps_x = ph1.enter_context(tc.psum_pool(name="ps_x", bufs=2))
+            ps_t = ph1.enter_context(tc.psum_pool(name="ps_t", bufs=2))
+            ps_e = ph1.enter_context(tc.psum_pool(name="ps_e", bufs=2))
             t_pool = ph1.enter_context(tc.tile_pool(name="t_pool", bufs=4))
             w_pool = ph1.enter_context(tc.tile_pool(name="w_pool", bufs=2))
             d_pool = ph1.enter_context(tc.tile_pool(name="d_pool", bufs=2))
             g_pool = ph1.enter_context(tc.tile_pool(name="g_pool", bufs=3))
-            t_of, xmt_of, mbv_of, dg_of, grp_of = {}, {}, {}, {}, {}
+            t_of, xmt_of, mbv_of, xt_of, esb_of, et_of, grp_of = {}, {}, {}, {}, {}, {}, {}
 
             def load(k):
                 t_in = t_pool.tile([P, J, BLK], BF16)
@@ -85,7 +84,8 @@ def tile_mixture_t_kernel(tc, inputs, biases, out):
             nc.gpsimd.tensor_tensor(out=js1[:], in0=sq[:, 0:2, :], in1=sq[:, 2:4, :], op=ALU.add)
             nc.gpsimd.tensor_tensor(out=js[:], in0=js1[:, 0, :], in1=js1[:, 1, :], op=ALU.add)
 
-            for it in range(NB + 3):
+            for it in range(NB + 4):
+                k1, k2, k3 = it - 1, it - 2, it - 3
                 if it < NB:
                     t_in = t_of[it]
                     a2 = w_pool.tile([P, 2, BLK], BF16)
@@ -97,50 +97,69 @@ def tile_mixture_t_kernel(tc, inputs, biases, out):
                         nc.tensor.transpose(xmt[:, i, :], xm[:, i * P : (i + 1) * P], ident[:])
                     xmt_of[it] = xmt
                 if it == 0:
-                    col_sum = ps_s.tile([P, 512], F32, tag="s")
+                    col_sum = ps_e.tile([P, 512], F32, tag="et")
                     nc.tensor.matmul(out=col_sum[:, 0:F], lhsT=ones[:], rhs=js[:], start=True, stop=True)
-                k = it - 1
-                if 0 <= k < NB:
+                if 0 <= k1 < NB:
                     with nc.allow_low_precision(reason="a maximum of bfloat16 values is a bfloat16 value"):
                         nc.vector.tensor_reduce(
-                            out=m_t[:, k * SUB : (k + 1) * SUB], in_=xmt_of[k][:], axis=AX.X, op=ALU.max
+                            out=m_t[:, k1 * SUB : (k1 + 1) * SUB], in_=xmt_of[k1][:], axis=AX.X, op=ALU.max
                         )
+                    nc.vector.tensor_scalar_mul(
+                        out=neg_m[:, k1, :], in0=m_t[:, k1 * SUB : k1 * SUB + NBG], scalar1=-1.0
+                    )
                     mb_v = ps_v.tile([P, BLK], BF16)
-                    mb_g = ps_g.tile([P, BLK], BF16)
-                    bcast(k, 0, mb_v, mb_g)
-                    mbv_of[k] = mb_v
-                k2 = it - 2
+                    bcast(k1, NBG, mb_v)
+                    mbv_of[k1] = mb_v
                 if 0 <= k2 < NB:
+                    e_sb = d_pool.tile([P, NBG, C], BF16)
+                    for g in range(NBG):
+                        nc.scalar.activation(
+                            out=e_sb[:, g, :],
+                            in_=xt_of[k2][g // 2][:, g % 2, :],
+                            func=ACT.Exp,
+                            bias=neg_m[:, k2, g : g + 1],
+                        )
+                    esb_of[k2] = e_sb
+                if 0 <= k1 < NB:
+                    xt_of[k1] = []
+                    for t in range(NBG // 2):
+                        xt = ps_t.tile([P, 2, C], BF16)
+                        for g in (2 * t, 2 * t + 1):
+                            for j in range(J):
+                                nc.tensor.transpose(
+                                    xt[:, g % 2, j * P : (j + 1) * P], t_of[k1][:, j, g * P : (g + 1) * P], ident[:]
+                                )
+                        xt_of[k1].append(xt)
+                if 0 <= k3 < NB:
+                    for t in range(NBG // 2):
+                        nc.scalar.copy(
+                            out=grp_of[k3][:, t * 1024 : (t + 1) * 1024].rearrange("p (g w j) -> p g w j", g=2, j=J),
+                            in_=et_of[k3][t][:].rearrange("p g j w -> p g w j"),
+                        )
+                if 0 <= k2 < NB:
+                    et_of[k2] = []
+                    for t in range(NBG // 2):
+                        et = ps_e.tile([P, 2, J, P], BF16)
+                        for g in (2 * t, 2 * t + 1):
+                            for j in range(J):
+                                nc.tensor.transpose(
+                                    et[:, g % 2, j, :], esb_of[k2][:, g, j * P : (j + 1) * P], ident[:]
+                                )
+                        et_of[k2].append(et)
+                    d_v = d_pool.tile([P, AW, J], F32)
+                    nc.vector.tensor_tensor(
+                        out=d_v[:],
+                        in0=t_of[k2][:, :, BW:BLK].rearrange("p j w -> p w j"),
+                        in1=mbv_of[k2][:, BW:BLK].unsqueeze(2).to_broadcast([P, AW, J]),
+                        op=ALU.subtract,
+                    )
                     grp = g_pool.tile([P, BLK * J], BF16, align_bytes=64)
                     grp_of[k2] = grp
                     nc.scalar.activation(
-                        out=grp[:, 0 : GW * J], in_=dg_of[k2][:].rearrange("p w j -> p (w j)"), func=ACT.Exp
-                    )
-                if 0 <= k < NB:
-                    nc.scalar.copy(out=mbs[:, k, :], in_=mb_g[:, 0:GW])
-                    d_g = d_pool.tile([P, GW, J], F32)
-                    for i in range(GS):
-                        nc.gpsimd.tensor_tensor(
-                            out=d_g[:, i * P : (i + 1) * P, :],
-                            in0=t_of[k][:, :, i * P : (i + 1) * P].rearrange("p j w -> p w j"),
-                            in1=mbs[:, k, i * P : (i + 1) * P].unsqueeze(2).to_broadcast([P, P, J]),
-                            op=ALU.subtract,
-                        )
-                    dg_of[k] = d_g
-                if 0 <= k2 < NB:
-                    d_v = d_pool.tile([P, VW, J], F32)
-                    nc.vector.tensor_tensor(
-                        out=d_v[:],
-                        in0=t_of[k2][:, :, GW:BLK].rearrange("p j w -> p w j"),
-                        in1=mbv_of[k2][:, GW:BLK].unsqueeze(2).to_broadcast([P, VW, J]),
-                        op=ALU.subtract,
-                    )
-                    nc.scalar.activation(
-                        out=grp_of[k2][:, GW * J : BLK * J], in_=d_v[:].rearrange("p w j -> p (w j)"), func=ACT.Exp
+                        out=grp[:, BW * J : BLK * J], in_=d_v[:].rearrange("p w j -> p (w j)"), func=ACT.Exp
                     )
                 if it + 2 < NB:
                     load(it + 2)
-                k3 = it - 3
                 if 0 <= k3 < NB:
                     nc.vector.quantize_mx(
                         out=codes[:, k3 * BLK : (k3 + 1) * BLK].bitcast(FP8X4),
@@ -163,16 +182,17 @@ def tile_mixture_t_kernel(tc, inputs, biases, out):
                     )
 
         with ExitStack() as ph2:
+            ps_s = ph2.enter_context(tc.psum_pool(name="ps_s", bufs=4))
             o_pool = ph2.enter_context(tc.tile_pool(name="o_pool", bufs=3))
             for k in range(NB):
                 mb_v = ps_v.tile([P, BLK], BF16)
-                bcast(k, GS, mb_v, mb_v)
+                bcast(k, 0, mb_v)
                 px = (k % 4) * BLK
                 for ft in range(2):
                     o_t = o_pool.tile([P, BLK], F32, tag="o%d" % ft)
                     for h in range(2):
                         cols = slice(k * BLK + h * 512, k * BLK + (h + 1) * 512)
-                        s = ps_s.tile([P, 512], F32, tag="s")
+                        s = ps_s.tile([P, 512], F32)
                         nc.tensor.matmul_mx(
                             out=s[:],
                             lhsT=p_codes[:, ft * P : (ft + 1) * P].bitcast(FP8X4),
@@ -183,8 +203,5 @@ def tile_mixture_t_kernel(tc, inputs, biases, out):
                             stop=True,
                         )
                         nc.scalar.activation(out=o_t[:, h * 512 : (h + 1) * 512], in_=s[:], func=ACT.Ln)
-                    nc.gpsimd.tensor_tensor(out=o_t[:, 0:GW], in0=o_t[:, 0:GW], in1=mbs[:, k, :], op=ALU.add)
-                    nc.vector.tensor_tensor(
-                        out=o_t[:, GW:BLK], in0=o_t[:, GW:BLK], in1=mb_v[:, GW:BLK], op=ALU.add
-                    )
+                    nc.vector.tensor_tensor(out=o_t[:], in0=o_t[:], in1=mb_v[:], op=ALU.add)
                     nc.sync.dma_start(out=o[k // 4, ft, :, px : px + BLK], in_=o_t[:])

@@ -15,32 +15,34 @@ AX = mybir.AxisListType
 P = 128
 B, C, HW, F = 4, 512, 4096, 256
 J = 4
+NPX = B * HW
+NGRP = NPX // P
 BLK = 1024
-NB = B * HW // BLK
 SUB = BLK // P
-NBG = 4
-BW = NBG * P
-AW = BLK - BW
 FLOPS = 2 * B * HW * C * F
 
 
 def tile_mixture_t_kernel(tc, inputs, biases, out):
     nc = tc.nc
+    BLOCKS = [(4, 2), (4, 2)] + [(8, 4 if i % 2 == 0 else 3) for i in range(15)]
+    OUT_BLOCKS = [8] * 15 + [4, 4]
     x = inputs.rearrange("b (p j) h w -> b p j (h w)", j=J)
     bia = biases[0, 0].rearrange("(p j) f -> p j f", j=J)
     o = out.rearrange("b (t f) h w -> b t f (h w)", t=2)
+    nb = len(BLOCKS)
+    g0_of = [sum([b[0] for b in BLOCKS[:k]]) for k in range(nb)]
+    assert g0_of[-1] + BLOCKS[-1][0] == NGRP and sum(OUT_BLOCKS) == NGRP
 
     with ExitStack() as ctx:
         ctx.enter_context(tc.manual_schedule())
         keep = ctx.enter_context(tc.tile_pool(name="keep", bufs=1))
-        ps_v = ctx.enter_context(tc.psum_pool(name="ps_v", bufs=2))
 
         ident = keep.tile([P, P], BF16)
         ones = keep.tile([P, P], F32)
-        codes = keep.tile([P, B * HW], U32, align_bytes=64)
-        scales = keep.tile([P, B * HW], U8, align_bytes=64)
-        m_t = keep.tile([P, NB * SUB], BF16)
-        neg_m = keep.tile([P, NB, NBG], F32)
+        codes = keep.tile([P, NPX], U32, align_bytes=64)
+        scales = keep.tile([P, NPX], U8, align_bytes=64)
+        m_t = keep.tile([P, NGRP], BF16)
+        neg_m = keep.tile([P, NGRP], F32)
         b_raw = keep.tile([P, J, F], BF16)
         sq = keep.tile([P, J, F], F32)
         js1 = keep.tile([P, 2, F], F32)
@@ -50,123 +52,144 @@ def tile_mixture_t_kernel(tc, inputs, biases, out):
         p_codes = keep.tile([P, F], U32, align_bytes=64)
         p_scales = keep.tile([P, F], U8, align_bytes=64)
 
-        nc.sync.dma_start(out=b_raw[:], in_=bia)
         make_identity(nc, ident[:])
         nc.gpsimd.memset(ones[:], 1.0)
 
-        def bcast(k, first, mb_v):
-            for i in range(first, SUB):
+        def bcast(g0, first, last, mb_v):
+            for i in range(first, last):
                 nc.tensor.transpose(
-                    mb_v[:, i * P : (i + 1) * P],
-                    m_t[:, k * SUB + i : k * SUB + i + 1].to_broadcast([P, P]),
-                    ident[:],
+                    mb_v[:, i * P : (i + 1) * P], m_t[:, g0 + i : g0 + i + 1].to_broadcast([P, P]), ident[:]
                 )
 
         with ExitStack() as ph1:
+            ps_v = ph1.enter_context(tc.psum_pool(name="ps_v", bufs=2))
             ps_x = ph1.enter_context(tc.psum_pool(name="ps_x", bufs=2))
             ps_t = ph1.enter_context(tc.psum_pool(name="ps_t", bufs=2))
             ps_e = ph1.enter_context(tc.psum_pool(name="ps_e", bufs=2))
             t_pool = ph1.enter_context(tc.tile_pool(name="t_pool", bufs=4))
             w_pool = ph1.enter_context(tc.tile_pool(name="w_pool", bufs=2))
-            d_pool = ph1.enter_context(tc.tile_pool(name="d_pool", bufs=2))
-            g_pool = ph1.enter_context(tc.tile_pool(name="g_pool", bufs=3))
-            t_of, xmt_of, mbv_of, xt_of, esb_of, et_of, grp_of = {}, {}, {}, {}, {}, {}, {}
+            d_pool = ph1.enter_context(tc.tile_pool(name="d_pool", bufs=3))
+            e_pool = ph1.enter_context(tc.tile_pool(name="e_pool", bufs=3))
+            g_pool = ph1.enter_context(tc.tile_pool(name="g_pool", bufs=4))
+            t_of, xmt_of, mbv_of, xt_of, esb_of, et_of, grp_of, dv_of = {}, {}, {}, {}, {}, {}, {}, {}
 
             def load(k):
                 t_in = t_pool.tile([P, J, BLK], BF16)
-                px = (k % 4) * BLK
-                nc.sync.dma_start(out=t_in[:], in_=x[k // 4, :, :, px : px + BLK])
+                w = BLOCKS[k][0] * P
+                px = g0_of[k] * P
+                nc.sync.dma_start(out=t_in[:, :, 0:w], in_=x[px // HW, :, :, px % HW : px % HW + w])
                 t_of[k] = t_in
 
             load(0)
             load(1)
+            nc.sync.dma_start(out=b_raw[:], in_=bia)
             nc.scalar.activation(out=sq[:], in_=b_raw[:], func=ACT.Square)
             nc.gpsimd.tensor_tensor(out=js1[:], in0=sq[:, 0:2, :], in1=sq[:, 2:4, :], op=ALU.add)
             nc.gpsimd.tensor_tensor(out=js[:], in0=js1[:, 0, :], in1=js1[:, 1, :], op=ALU.add)
 
-            for it in range(NB + 4):
-                k1, k2, k3 = it - 1, it - 2, it - 3
-                if it < NB:
+            for it in range(nb + 5):
+                k1, k2, k3, k4, k5 = it - 1, it - 2, it - 3, it - 4, it - 5
+                if it < nb:
+                    ng = BLOCKS[it][0]
+                    w = ng * P
                     t_in = t_of[it]
                     a2 = w_pool.tile([P, 2, BLK], BF16)
                     xm = w_pool.tile([P, BLK], BF16)
-                    nc.vector.tensor_tensor(out=a2[:], in0=t_in[:, 0:2, :], in1=t_in[:, 2:4, :], op=ALU.max)
-                    nc.vector.tensor_tensor(out=xm[:], in0=a2[:, 0, :], in1=a2[:, 1, :], op=ALU.max)
+                    nc.vector.tensor_tensor(
+                        out=a2[:, :, 0:w], in0=t_in[:, 0:2, 0:w], in1=t_in[:, 2:4, 0:w], op=ALU.max
+                    )
+                    nc.vector.tensor_tensor(out=xm[:, 0:w], in0=a2[:, 0, 0:w], in1=a2[:, 1, 0:w], op=ALU.max)
                     xmt = ps_x.tile([P, SUB, P], BF16)
-                    for i in range(SUB):
+                    for i in range(ng):
                         nc.tensor.transpose(xmt[:, i, :], xm[:, i * P : (i + 1) * P], ident[:])
                     xmt_of[it] = xmt
-                if it == 0:
-                    col_sum = ps_e.tile([P, 512], F32, tag="et")
-                    nc.tensor.matmul(out=col_sum[:, 0:F], lhsT=ones[:], rhs=js[:], start=True, stop=True)
-                if 0 <= k1 < NB:
-                    with nc.allow_low_precision(reason="a maximum of bfloat16 values is a bfloat16 value"):
-                        nc.vector.tensor_reduce(
-                            out=m_t[:, k1 * SUB : (k1 + 1) * SUB], in_=xmt_of[k1][:], axis=AX.X, op=ALU.max
+                if 0 <= k4 < nb:
+                    nbg = BLOCKS[k4][1]
+                    for t in range((nbg + 1) // 2):
+                        n = min(2, nbg - 2 * t)
+                        nc.scalar.copy(
+                            out=grp_of[k4][:, t * 1024 : t * 1024 + n * 512].rearrange(
+                                "p (g w j) -> p g w j", g=n, j=J
+                            ),
+                            in_=et_of[k4][t][:, 0:n, :, :].rearrange("p g j w -> p g w j"),
                         )
-                    nc.vector.tensor_scalar_mul(
-                        out=neg_m[:, k1, :], in0=m_t[:, k1 * SUB : k1 * SUB + NBG], scalar1=-1.0
-                    )
-                    mb_v = ps_v.tile([P, BLK], BF16)
-                    bcast(k1, NBG, mb_v)
-                    mbv_of[k1] = mb_v
-                if 0 <= k2 < NB:
-                    e_sb = d_pool.tile([P, NBG, C], BF16)
-                    for g in range(NBG):
+                if 0 <= k3 < nb:
+                    nbg = BLOCKS[k3][1]
+                    et_of[k3] = []
+                    for t in range((nbg + 1) // 2):
+                        et = ps_e.tile([P, 2, J, P], BF16)
+                        for g in range(2 * t, min(2 * t + 2, nbg)):
+                            for j in range(J):
+                                nc.tensor.transpose(
+                                    et[:, g % 2, j, :], esb_of[k3][:, g, j * P : (j + 1) * P], ident[:]
+                                )
+                        et_of[k3].append(et)
+                if 0 <= k2 < nb:
+                    nbg = BLOCKS[k2][1]
+                    e_sb = e_pool.tile([P, 4, C], BF16)
+                    for g in range(nbg):
                         nc.scalar.activation(
                             out=e_sb[:, g, :],
                             in_=xt_of[k2][g // 2][:, g % 2, :],
                             func=ACT.Exp,
-                            bias=neg_m[:, k2, g : g + 1],
+                            bias=neg_m[:, g0_of[k2] + g : g0_of[k2] + g + 1],
                         )
                     esb_of[k2] = e_sb
-                if 0 <= k1 < NB:
+                if 0 <= k1 < nb:
+                    ng, nbg = BLOCKS[k1]
                     xt_of[k1] = []
-                    for t in range(NBG // 2):
+                    for t in range((nbg + 1) // 2):
                         xt = ps_t.tile([P, 2, C], BF16)
-                        for g in (2 * t, 2 * t + 1):
+                        for g in range(2 * t, min(2 * t + 2, nbg)):
                             for j in range(J):
                                 nc.tensor.transpose(
                                     xt[:, g % 2, j * P : (j + 1) * P], t_of[k1][:, j, g * P : (g + 1) * P], ident[:]
                                 )
                         xt_of[k1].append(xt)
-                if 0 <= k3 < NB:
-                    for t in range(NBG // 2):
-                        nc.scalar.copy(
-                            out=grp_of[k3][:, t * 1024 : (t + 1) * 1024].rearrange("p (g w j) -> p g w j", g=2, j=J),
-                            in_=et_of[k3][t][:].rearrange("p g j w -> p g w j"),
+                    g0 = g0_of[k1]
+                    with nc.allow_low_precision(reason="a maximum of bfloat16 values is a bfloat16 value"):
+                        nc.vector.tensor_reduce(
+                            out=m_t[:, g0 : g0 + ng], in_=xmt_of[k1][:, 0:ng, :], axis=AX.X, op=ALU.max
                         )
-                if 0 <= k2 < NB:
-                    et_of[k2] = []
-                    for t in range(NBG // 2):
-                        et = ps_e.tile([P, 2, J, P], BF16)
-                        for g in (2 * t, 2 * t + 1):
-                            for j in range(J):
-                                nc.tensor.transpose(
-                                    et[:, g % 2, j, :], esb_of[k2][:, g, j * P : (j + 1) * P], ident[:]
-                                )
-                        et_of[k2].append(et)
-                    d_v = d_pool.tile([P, AW, J], F32)
+                    nc.vector.tensor_scalar_mul(out=neg_m[:, g0 : g0 + nbg], in0=m_t[:, g0 : g0 + nbg], scalar1=-1.0)
+                    mb_v = ps_v.tile([P, BLK], BF16)
+                    bcast(g0, nbg, ng, mb_v)
+                    mbv_of[k1] = mb_v
+                if 0 <= k3 < nb:
+                    ng, nbg = BLOCKS[k3]
+                    aw = (ng - nbg) * P
+                    grp = g_pool.tile([P, BLK * J], BF16, align_bytes=64)
+                    grp_of[k3] = grp
+                    nc.scalar.activation(
+                        out=grp[:, nbg * P * J : ng * P * J],
+                        in_=dv_of[k3][:, 0:aw, :].rearrange("p w j -> p (w j)"),
+                        func=ACT.Exp,
+                    )
+                if 0 <= k2 < nb:
+                    ng, nbg = BLOCKS[k2]
+                    aw = (ng - nbg) * P
+                    d_v = d_pool.tile([P, 5 * P, J], F32)
                     nc.vector.tensor_tensor(
-                        out=d_v[:],
-                        in0=t_of[k2][:, :, BW:BLK].rearrange("p j w -> p w j"),
-                        in1=mbv_of[k2][:, BW:BLK].unsqueeze(2).to_broadcast([P, AW, J]),
+                        out=d_v[:, 0:aw, :],
+                        in0=t_of[k2][:, :, nbg * P : ng * P].rearrange("p j w -> p w j"),
+                        in1=mbv_of[k2][:, nbg * P : ng * P].unsqueeze(2).to_broadcast([P, aw, J]),
                         op=ALU.subtract,
                     )
-                    grp = g_pool.tile([P, BLK * J], BF16, align_bytes=64)
-                    grp_of[k2] = grp
-                    nc.scalar.activation(
-                        out=grp[:, BW * J : BLK * J], in_=d_v[:].rearrange("p w j -> p (w j)"), func=ACT.Exp
-                    )
-                if it + 2 < NB:
+                    dv_of[k2] = d_v
+                if it + 2 < nb:
                     load(it + 2)
-                if 0 <= k3 < NB:
+                if 0 <= k5 < nb:
+                    c0 = g0_of[k5] * P
+                    w = BLOCKS[k5][0] * P
                     nc.vector.quantize_mx(
-                        out=codes[:, k3 * BLK : (k3 + 1) * BLK].bitcast(FP8X4),
-                        scales=scales[:, k3 * BLK : (k3 + 1) * BLK],
-                        in_=grp_of[k3][:],
+                        out=codes[:, c0 : c0 + w].bitcast(FP8X4),
+                        scales=scales[:, c0 : c0 + w],
+                        in_=grp_of[k5][:, 0 : w * J],
                     )
-                if it == 1:
+                if it == nb:
+                    col_sum = ps_x.tile([P, 512], F32, tag="xmt")
+                    nc.tensor.matmul(out=col_sum[:, 0:F], lhsT=ones[:], rhs=js[:], start=True, stop=True)
+                if it == nb + 1:
                     nc.vector.reciprocal(out=rs[:], in_=col_sum[:, 0:F])
                     nc.gpsimd.tensor_tensor(
                         out=p_grp[:],
@@ -174,7 +197,7 @@ def tile_mixture_t_kernel(tc, inputs, biases, out):
                         in1=rs[:].unsqueeze(2).to_broadcast([P, F, J]),
                         op=ALU.mult,
                     )
-                if it == 2:
+                if it == nb + 2:
                     nc.vector.quantize_mx(
                         out=p_codes[:].bitcast(FP8X4),
                         scales=p_scales[:],
@@ -182,16 +205,19 @@ def tile_mixture_t_kernel(tc, inputs, biases, out):
                     )
 
         with ExitStack() as ph2:
-            ps_s = ph2.enter_context(tc.psum_pool(name="ps_s", bufs=4))
-            o_pool = ph2.enter_context(tc.tile_pool(name="o_pool", bufs=3))
-            for k in range(NB):
-                mb_v = ps_v.tile([P, BLK], BF16)
-                bcast(k, 0, mb_v)
-                px = (k % 4) * BLK
+            ps_m = ph2.enter_context(tc.psum_pool(name="ps_m", bufs=3))
+            ps_s = ph2.enter_context(tc.psum_pool(name="ps_s", bufs=5))
+            o_pool = ph2.enter_context(tc.tile_pool(name="o_pool", bufs=4))
+            g0 = 0
+            for ng in OUT_BLOCKS:
+                w = ng * P
+                px = g0 * P
+                mb_v = ps_m.tile([P, BLK], BF16)
+                bcast(g0, 0, ng, mb_v)
                 for ft in range(2):
                     o_t = o_pool.tile([P, BLK], F32, tag="o%d" % ft)
-                    for h in range(2):
-                        cols = slice(k * BLK + h * 512, k * BLK + (h + 1) * 512)
+                    for h in range(w // 512):
+                        cols = slice(px + h * 512, px + (h + 1) * 512)
                         s = ps_s.tile([P, 512], F32)
                         nc.tensor.matmul_mx(
                             out=s[:],
@@ -203,5 +229,6 @@ def tile_mixture_t_kernel(tc, inputs, biases, out):
                             stop=True,
                         )
                         nc.scalar.activation(out=o_t[:, h * 512 : (h + 1) * 512], in_=s[:], func=ACT.Ln)
-                    nc.vector.tensor_tensor(out=o_t[:], in0=o_t[:], in1=mb_v[:], op=ALU.add)
-                    nc.sync.dma_start(out=o[k // 4, ft, :, px : px + BLK], in_=o_t[:])
+                    nc.vector.tensor_tensor(out=o_t[:, 0:w], in0=o_t[:, 0:w], in1=mb_v[:, 0:w], op=ALU.add)
+                    nc.sync.dma_start(out=o[px // HW, ft, :, px % HW : px % HW + w], in_=o_t[:, 0:w])
+                g0 += ng

@@ -24,8 +24,14 @@ FLOPS = 2 * B * HW * C * F
 
 def tile_mixture_t_kernel(tc, inputs, biases, out):
     nc = tc.nc
-    BLOCKS = [(4, 2), (4, 2)] + [(8, 4 if i % 2 == 0 else 3) for i in range(15)]
-    OUT_BLOCKS = [8] * 15 + [4, 4]
+    BLOCKS = (
+        [(2, 1, 0), (2, 1, 0), (4, 2, 0)]
+        + [(8, 3, 2)] * 5
+        + [(8, 3, 1)] * 6
+        + [(8, 2, 2)] * 3
+        + [(4, 1, 1), (4, 0, 1)]
+    )
+    OUT_BLOCKS = [8] * 15 + [4, 2, 2]
     x = inputs.rearrange("b (p j) h w -> b p j (h w)", j=J)
     bia = biases[0, 0].rearrange("(p j) f -> p j f", j=J)
     o = out.rearrange("b (t f) h w -> b t f (h w)", t=2)
@@ -41,8 +47,9 @@ def tile_mixture_t_kernel(tc, inputs, biases, out):
         ones = keep.tile([P, P], F32)
         codes = keep.tile([P, NPX], U32, align_bytes=64)
         scales = keep.tile([P, NPX], U8, align_bytes=64)
-        m_t = keep.tile([P, NGRP], BF16)
-        neg_m = keep.tile([P, NGRP], F32)
+        ident32 = keep.tile([P, P], F32)
+        nm16 = keep.tile([P, NGRP], BF16)
+        nm32 = keep.tile([P, NGRP], F32)
         b_raw = keep.tile([P, J, F], BF16)
         sq = keep.tile([P, J, F], F32)
         js1 = keep.tile([P, 2, F], F32)
@@ -53,17 +60,19 @@ def tile_mixture_t_kernel(tc, inputs, biases, out):
         p_scales = keep.tile([P, F], U8, align_bytes=64)
 
         make_identity(nc, ident[:])
+        make_identity(nc, ident32[:])
         nc.gpsimd.memset(ones[:], 1.0)
 
         def bcast(g0, first, last, mb_v):
             for i in range(first, last):
                 nc.tensor.transpose(
-                    mb_v[:, i * P : (i + 1) * P], m_t[:, g0 + i : g0 + i + 1].to_broadcast([P, P]), ident[:]
+                    mb_v[:, i * P : (i + 1) * P], nm16[:, g0 + i : g0 + i + 1].to_broadcast([P, P]), ident[:]
                 )
 
         with ExitStack() as ph1:
-            ps_v = ph1.enter_context(tc.psum_pool(name="ps_v", bufs=2))
-            ps_x = ph1.enter_context(tc.psum_pool(name="ps_x", bufs=2))
+            ps_v = ph1.enter_context(tc.psum_pool(name="ps_v", bufs=1))
+            ps_x = ph1.enter_context(tc.psum_pool(name="ps_x", bufs=1))
+            ps_f = ph1.enter_context(tc.psum_pool(name="ps_f", bufs=2))
             ps_t = ph1.enter_context(tc.psum_pool(name="ps_t", bufs=2))
             ps_e = ph1.enter_context(tc.psum_pool(name="ps_e", bufs=2))
             t_pool = ph1.enter_context(tc.tile_pool(name="t_pool", bufs=4))
@@ -71,7 +80,7 @@ def tile_mixture_t_kernel(tc, inputs, biases, out):
             d_pool = ph1.enter_context(tc.tile_pool(name="d_pool", bufs=3))
             e_pool = ph1.enter_context(tc.tile_pool(name="e_pool", bufs=3))
             g_pool = ph1.enter_context(tc.tile_pool(name="g_pool", bufs=4))
-            t_of, xmt_of, mbv_of, xt_of, esb_of, et_of, grp_of, dv_of = {}, {}, {}, {}, {}, {}, {}, {}
+            t_of, xmt_of, mbv_of, xt_of, esb_of, et_of, grp_of, dv_of, df_of = {}, {}, {}, {}, {}, {}, {}, {}, {}
 
             def load(k):
                 t_in = t_pool.tile([P, J, BLK], BF16)
@@ -83,26 +92,9 @@ def tile_mixture_t_kernel(tc, inputs, biases, out):
             load(0)
             load(1)
             nc.sync.dma_start(out=b_raw[:], in_=bia)
-            nc.scalar.activation(out=sq[:], in_=b_raw[:], func=ACT.Square)
-            nc.gpsimd.tensor_tensor(out=js1[:], in0=sq[:, 0:2, :], in1=sq[:, 2:4, :], op=ALU.add)
-            nc.gpsimd.tensor_tensor(out=js[:], in0=js1[:, 0, :], in1=js1[:, 1, :], op=ALU.add)
 
             for it in range(nb + 5):
                 k1, k2, k3, k4, k5 = it - 1, it - 2, it - 3, it - 4, it - 5
-                if it < nb:
-                    ng = BLOCKS[it][0]
-                    w = ng * P
-                    t_in = t_of[it]
-                    a2 = w_pool.tile([P, 2, BLK], BF16)
-                    xm = w_pool.tile([P, BLK], BF16)
-                    nc.vector.tensor_tensor(
-                        out=a2[:, :, 0:w], in0=t_in[:, 0:2, 0:w], in1=t_in[:, 2:4, 0:w], op=ALU.max
-                    )
-                    nc.vector.tensor_tensor(out=xm[:, 0:w], in0=a2[:, 0, 0:w], in1=a2[:, 1, 0:w], op=ALU.max)
-                    xmt = ps_x.tile([P, SUB, P], BF16)
-                    for i in range(ng):
-                        nc.tensor.transpose(xmt[:, i, :], xm[:, i * P : (i + 1) * P], ident[:])
-                    xmt_of[it] = xmt
                 if 0 <= k4 < nb:
                     nbg = BLOCKS[k4][1]
                     for t in range((nbg + 1) // 2):
@@ -124,19 +116,41 @@ def tile_mixture_t_kernel(tc, inputs, biases, out):
                                     et[:, g % 2, j, :], esb_of[k3][:, g, j * P : (j + 1) * P], ident[:]
                                 )
                         et_of[k3].append(et)
+                if 0 <= k1 < nb:
+                    ng = BLOCKS[k1][0]
+                    g0 = g0_of[k1]
+                    nc.vector.tensor_reduce(
+                        out=nm32[:, g0 : g0 + ng], in_=xmt_of[k1][:, 0:ng, :], axis=AX.X, op=ALU.max, negate=True
+                    )
+                    nc.gpsimd.tensor_copy(out=nm16[:, g0 : g0 + ng], in_=nm32[:, g0 : g0 + ng])
+                if it < nb:
+                    ng = BLOCKS[it][0]
+                    w = ng * P
+                    t_in = t_of[it]
+                    a2 = w_pool.tile([P, 2, BLK], BF16)
+                    xm = w_pool.tile([P, BLK], BF16)
+                    nc.vector.tensor_tensor(
+                        out=a2[:, :, 0:w], in0=t_in[:, 0:2, 0:w], in1=t_in[:, 2:4, 0:w], op=ALU.max
+                    )
+                    nc.vector.tensor_tensor(out=xm[:, 0:w], in0=a2[:, 0, 0:w], in1=a2[:, 1, 0:w], op=ALU.max)
+                    xmt = ps_x.tile([P, SUB, P], BF16)
+                    for i in range(ng):
+                        nc.tensor.transpose(xmt[:, i, :], xm[:, i * P : (i + 1) * P], ident[:])
+                    xmt_of[it] = xmt
                 if 0 <= k2 < nb:
                     nbg = BLOCKS[k2][1]
-                    e_sb = e_pool.tile([P, 4, C], BF16)
+                    if nbg > 0:
+                        e_sb = e_pool.tile([P, 4, C], BF16)
+                        esb_of[k2] = e_sb
                     for g in range(nbg):
                         nc.scalar.activation(
-                            out=e_sb[:, g, :],
+                            out=esb_of[k2][:, g, :],
                             in_=xt_of[k2][g // 2][:, g % 2, :],
                             func=ACT.Exp,
-                            bias=neg_m[:, g0_of[k2] + g : g0_of[k2] + g + 1],
+                            bias=nm32[:, g0_of[k2] + g : g0_of[k2] + g + 1],
                         )
-                    esb_of[k2] = e_sb
                 if 0 <= k1 < nb:
-                    ng, nbg = BLOCKS[k1]
+                    nbg = BLOCKS[k1][1]
                     xt_of[k1] = []
                     for t in range((nbg + 1) // 2):
                         xt = ps_t.tile([P, 2, C], BF16)
@@ -146,36 +160,63 @@ def tile_mixture_t_kernel(tc, inputs, biases, out):
                                     xt[:, g % 2, j * P : (j + 1) * P], t_of[k1][:, j, g * P : (g + 1) * P], ident[:]
                                 )
                         xt_of[k1].append(xt)
-                    g0 = g0_of[k1]
-                    with nc.allow_low_precision(reason="a maximum of bfloat16 values is a bfloat16 value"):
-                        nc.vector.tensor_reduce(
-                            out=m_t[:, g0 : g0 + ng], in_=xmt_of[k1][:, 0:ng, :], axis=AX.X, op=ALU.max
-                        )
-                    nc.vector.tensor_scalar_mul(out=neg_m[:, g0 : g0 + nbg], in0=m_t[:, g0 : g0 + nbg], scalar1=-1.0)
-                    mb_v = ps_v.tile([P, BLK], BF16)
-                    bcast(g0, nbg, ng, mb_v)
-                    mbv_of[k1] = mb_v
                 if 0 <= k3 < nb:
-                    ng, nbg = BLOCKS[k3]
-                    aw = (ng - nbg) * P
+                    ng, nbg, nfg = BLOCKS[k3]
                     grp = g_pool.tile([P, BLK * J], BF16, align_bytes=64)
                     grp_of[k3] = grp
+                    for f in range(nfg):
+                        g = nbg + f
+                        nc.scalar.activation(
+                            out=grp[:, g * 512 : (g + 1) * 512].rearrange("p (w j) -> p w j", j=J),
+                            in_=df_of[k3][f][:].rearrange("p j w -> p w j"),
+                            func=ACT.Exp,
+                        )
+                if 0 <= k2 < nb:
+                    ng, nbg, nfg = BLOCKS[k2]
+                    df_of[k2] = []
+                    for f in range(nfg):
+                        g = nbg + f
+                        col = g0_of[k2] + g
+                        df = ps_f.tile([P, J, P], F32)
+                        nc.tensor.matmul(
+                            out=df[:], lhsT=ident[:], rhs=t_of[k2][:, :, g * P : (g + 1) * P], start=True, stop=False
+                        )
+                        for j in range(J):
+                            nc.tensor.matmul(
+                                out=df[:, j, :],
+                                lhsT=nm32[:, col : col + 1].to_broadcast([P, P]),
+                                rhs=ident32[:],
+                                is_transpose=True,
+                                start=False,
+                                stop=(j == J - 1),
+                            )
+                        df_of[k2].append(df)
+                if 0 <= k3 < nb:
+                    ng, nbg, nfg = BLOCKS[k3]
+                    a0 = nbg + nfg
+                    aw = (ng - a0) * P
                     nc.scalar.activation(
-                        out=grp[:, nbg * P * J : ng * P * J],
+                        out=grp_of[k3][:, a0 * P * J : ng * P * J],
                         in_=dv_of[k3][:, 0:aw, :].rearrange("p w j -> p (w j)"),
                         func=ACT.Exp,
                     )
                 if 0 <= k2 < nb:
-                    ng, nbg = BLOCKS[k2]
-                    aw = (ng - nbg) * P
-                    d_v = d_pool.tile([P, 5 * P, J], F32)
+                    ng, nbg, nfg = BLOCKS[k2]
+                    a0 = nbg + nfg
+                    aw = (ng - a0) * P
+                    d_v = d_pool.tile([P, 4 * P, J], F32)
                     nc.vector.tensor_tensor(
                         out=d_v[:, 0:aw, :],
-                        in0=t_of[k2][:, :, nbg * P : ng * P].rearrange("p j w -> p w j"),
-                        in1=mbv_of[k2][:, nbg * P : ng * P].unsqueeze(2).to_broadcast([P, aw, J]),
-                        op=ALU.subtract,
+                        in0=t_of[k2][:, :, a0 * P : ng * P].rearrange("p j w -> p w j"),
+                        in1=mbv_of[k2][:, a0 * P : ng * P].unsqueeze(2).to_broadcast([P, aw, J]),
+                        op=ALU.add,
                     )
                     dv_of[k2] = d_v
+                if 0 <= k1 < nb:
+                    ng, nbg, nfg = BLOCKS[k1]
+                    mb_v = ps_v.tile([P, BLK], BF16)
+                    bcast(g0_of[k1], nbg + nfg, ng, mb_v)
+                    mbv_of[k1] = mb_v
                 if it + 2 < nb:
                     load(it + 2)
                 if 0 <= k5 < nb:
@@ -186,6 +227,10 @@ def tile_mixture_t_kernel(tc, inputs, biases, out):
                         scales=scales[:, c0 : c0 + w],
                         in_=grp_of[k5][:, 0 : w * J],
                     )
+                if it == 5:
+                    nc.scalar.activation(out=sq[:], in_=b_raw[:], func=ACT.Square)
+                    nc.gpsimd.tensor_tensor(out=js1[:], in0=sq[:, 0:2, :], in1=sq[:, 2:4, :], op=ALU.add)
+                    nc.gpsimd.tensor_tensor(out=js[:], in0=js1[:, 0, :], in1=js1[:, 1, :], op=ALU.add)
                 if it == nb:
                     col_sum = ps_x.tile([P, 512], F32, tag="xmt")
                     nc.tensor.matmul(out=col_sum[:, 0:F], lhsT=ones[:], rhs=js[:], start=True, stop=True)
@@ -216,11 +261,12 @@ def tile_mixture_t_kernel(tc, inputs, biases, out):
                 bcast(g0, 0, ng, mb_v)
                 for ft in range(2):
                     o_t = o_pool.tile([P, BLK], F32, tag="o%d" % ft)
-                    for h in range(w // 512):
-                        cols = slice(px + h * 512, px + (h + 1) * 512)
+                    for c0 in range(0, w, 512):
+                        cw = min(512, w - c0)
+                        cols = slice(px + c0, px + c0 + cw)
                         s = ps_s.tile([P, 512], F32)
                         nc.tensor.matmul_mx(
-                            out=s[:],
+                            out=s[:, 0:cw],
                             lhsT=p_codes[:, ft * P : (ft + 1) * P].bitcast(FP8X4),
                             lhsT_scale=p_scales[:, ft * P : (ft + 1) * P],
                             rhs=codes[:, cols].bitcast(FP8X4),
@@ -228,7 +274,7 @@ def tile_mixture_t_kernel(tc, inputs, biases, out):
                             start=True,
                             stop=True,
                         )
-                        nc.scalar.activation(out=o_t[:, h * 512 : (h + 1) * 512], in_=s[:], func=ACT.Ln)
-                    nc.vector.tensor_tensor(out=o_t[:, 0:w], in0=o_t[:, 0:w], in1=mb_v[:, 0:w], op=ALU.add)
+                        nc.scalar.activation(out=o_t[:, c0 : c0 + cw], in_=s[:, 0:cw], func=ACT.Ln)
+                    nc.vector.tensor_tensor(out=o_t[:, 0:w], in0=o_t[:, 0:w], in1=mb_v[:, 0:w], op=ALU.subtract)
                     nc.sync.dma_start(out=o[px // HW, ft, :, px % HW : px % HW + w], in_=o_t[:, 0:w])
                 g0 += ng

@@ -25,11 +25,10 @@ FLOPS = 2 * B * HW * C * F
 def tile_mixture_t_kernel(tc, inputs, biases, out):
     nc = tc.nc
     BLOCKS = (
-        [(2, 1, 0), (2, 1, 0), (4, 2, 0)]
-        + [(8, 3, 2)] * 5
-        + [(8, 3, 1)] * 6
-        + [(8, 2, 2)] * 3
-        + [(4, 1, 1), (4, 0, 1)]
+        [(2, 2, 0), (2, 0, 0), (4, 2, 0)]
+        + [(8, 4, 1), (8, 2, 2)] * 6
+        + [(8, 2, 2), (8, 2, 1)]
+        + [(4, 0, 2), (4, 0, 1)]
     )
     OUT_BLOCKS = [8] * 15 + [4, 2, 2]
     x = inputs.rearrange("b (p j) h w -> b p j (h w)", j=J)
@@ -120,7 +119,11 @@ def tile_mixture_t_kernel(tc, inputs, biases, out):
                     ng = BLOCKS[k1][0]
                     g0 = g0_of[k1]
                     nc.vector.tensor_reduce(
-                        out=nm32[:, g0 : g0 + ng], in_=xmt_of[k1][:, 0:ng, :], axis=AX.X, op=ALU.max, negate=True
+                        out=nm32[:, g0 : g0 + ng].rearrange("q (g e) -> q g e", e=2),
+                        in_=xmt_of[k1][:].bitcast(BF16).rearrange("q (g p e) -> q g e p", p=P, e=2)[:, 0 : ng // 2, :, :],
+                        axis=AX.X,
+                        op=ALU.max,
+                        negate=True,
                     )
                     nc.gpsimd.tensor_copy(out=nm16[:, g0 : g0 + ng], in_=nm32[:, g0 : g0 + ng])
                 if it < nb:
@@ -133,9 +136,11 @@ def tile_mixture_t_kernel(tc, inputs, biases, out):
                         out=a2[:, :, 0:w], in0=t_in[:, 0:2, 0:w], in1=t_in[:, 2:4, 0:w], op=ALU.max
                     )
                     nc.vector.tensor_tensor(out=xm[:, 0:w], in0=a2[:, 0, 0:w], in1=a2[:, 1, 0:w], op=ALU.max)
-                    xmt = ps_x.tile([P, SUB, P], BF16)
-                    for i in range(ng):
-                        nc.tensor.transpose(xmt[:, i, :], xm[:, i * P : (i + 1) * P], ident[:])
+                    xmt = ps_x.tile([P, 512], F32)
+                    for i in range(ng // 2):
+                        nc.tensor.transpose(
+                            xmt[:, i * P : (i + 1) * P], xm[:].bitcast(F32)[:, i * P : (i + 1) * P], ident32[:]
+                        )
                     xmt_of[it] = xmt
                 if 0 <= k2 < nb:
                     nbg = BLOCKS[k2][1]
@@ -145,20 +150,21 @@ def tile_mixture_t_kernel(tc, inputs, biases, out):
                     for g in range(nbg):
                         nc.scalar.activation(
                             out=esb_of[k2][:, g, :],
-                            in_=xt_of[k2][g // 2][:, g % 2, :],
+                            in_=xt_of[k2][g // 2][:].bitcast(BF16).rearrange("q (c e) -> q e c", e=2)[:, g % 2, :],
                             func=ACT.Exp,
                             bias=nm32[:, g0_of[k2] + g : g0_of[k2] + g + 1],
                         )
                 if 0 <= k1 < nb:
                     nbg = BLOCKS[k1][1]
                     xt_of[k1] = []
-                    for t in range((nbg + 1) // 2):
-                        xt = ps_t.tile([P, 2, C], BF16)
-                        for g in range(2 * t, min(2 * t + 2, nbg)):
-                            for j in range(J):
-                                nc.tensor.transpose(
-                                    xt[:, g % 2, j * P : (j + 1) * P], t_of[k1][:, j, g * P : (g + 1) * P], ident[:]
-                                )
+                    for t in range(nbg // 2):
+                        xt = ps_t.tile([P, C], F32)
+                        for j in range(J):
+                            nc.tensor.transpose(
+                                xt[:, j * P : (j + 1) * P],
+                                t_of[k1][:, j, :].bitcast(F32)[:, t * P : (t + 1) * P],
+                                ident32[:],
+                            )
                         xt_of[k1].append(xt)
                 if 0 <= k3 < nb:
                     ng, nbg, nfg = BLOCKS[k3]
@@ -178,8 +184,13 @@ def tile_mixture_t_kernel(tc, inputs, biases, out):
                         g = nbg + f
                         col = g0_of[k2] + g
                         df = ps_f.tile([P, J, P], F32)
+                        pair = t_of[k2][:, :, (g // 2) * 256 : (g // 2 + 1) * 256]
                         nc.tensor.matmul(
-                            out=df[:], lhsT=ident[:], rhs=t_of[k2][:, :, g * P : (g + 1) * P], start=True, stop=False
+                            out=df[:],
+                            lhsT=ident[:],
+                            rhs=pair.rearrange("p j (q e) -> p j q e", e=2)[:, :, :, g % 2],
+                            start=True,
+                            stop=False,
                         )
                         for j in range(J):
                             nc.tensor.matmul(
@@ -195,28 +206,47 @@ def tile_mixture_t_kernel(tc, inputs, biases, out):
                     ng, nbg, nfg = BLOCKS[k3]
                     a0 = nbg + nfg
                     aw = (ng - a0) * P
-                    nc.scalar.activation(
-                        out=grp_of[k3][:, a0 * P * J : ng * P * J],
-                        in_=dv_of[k3][:, 0:aw, :].rearrange("p w j -> p (w j)"),
-                        func=ACT.Exp,
-                    )
+                    if aw > 0:
+                        nc.scalar.activation(
+                            out=grp_of[k3][:, a0 * P * J : ng * P * J],
+                            in_=dv_of[k3][:, 0:aw, :].rearrange("p w j -> p (w j)"),
+                            func=ACT.Exp,
+                        )
                 if 0 <= k2 < nb:
                     ng, nbg, nfg = BLOCKS[k2]
                     a0 = nbg + nfg
                     aw = (ng - a0) * P
-                    d_v = d_pool.tile([P, 4 * P, J], F32)
-                    nc.vector.tensor_tensor(
-                        out=d_v[:, 0:aw, :],
-                        in0=t_of[k2][:, :, a0 * P : ng * P].rearrange("p j w -> p w j"),
-                        in1=mbv_of[k2][:, a0 * P : ng * P].unsqueeze(2).to_broadcast([P, aw, J]),
-                        op=ALU.add,
-                    )
-                    dv_of[k2] = d_v
+                    if aw > 0:
+                        d_v = d_pool.tile([P, 5 * P, J], F32)
+                        dv_of[k2] = d_v
+                    g = a0
+                    while g < ng:
+                        pair = t_of[k2][:, :, (g // 2) * 256 : (g // 2 + 1) * 256].rearrange("p j (q e) -> p e q j", e=2)
+                        if g % 2 == 1:
+                            nc.vector.tensor_tensor(
+                                out=d_v[:, (g - a0) * P : (g - a0 + 1) * P, :],
+                                in0=pair[:, 1, :, :],
+                                in1=mbv_of[k2][:, g * P : (g + 1) * P].unsqueeze(2).to_broadcast([P, P, J]),
+                                op=ALU.add,
+                            )
+                            g += 1
+                        else:
+                            nc.vector.tensor_tensor(
+                                out=d_v[:, (g - a0) * P : (g - a0 + 2) * P, :].rearrange("p (e q) j -> p e q j", e=2),
+                                in0=pair,
+                                in1=mbv_of[k2][:, g * P : (g + 2) * P]
+                                .rearrange("p (e q) -> p e q", e=2)
+                                .unsqueeze(3)
+                                .to_broadcast([P, 2, P, J]),
+                                op=ALU.add,
+                            )
+                            g += 2
                 if 0 <= k1 < nb:
                     ng, nbg, nfg = BLOCKS[k1]
-                    mb_v = ps_v.tile([P, BLK], BF16)
-                    bcast(g0_of[k1], nbg + nfg, ng, mb_v)
-                    mbv_of[k1] = mb_v
+                    if nbg + nfg < ng:
+                        mb_v = ps_v.tile([P, BLK], BF16)
+                        bcast(g0_of[k1], nbg + nfg, ng, mb_v)
+                        mbv_of[k1] = mb_v
                 if it + 2 < nb:
                     load(it + 2)
                 if 0 <= k5 < nb:
@@ -253,6 +283,7 @@ def tile_mixture_t_kernel(tc, inputs, biases, out):
             ps_m = ph2.enter_context(tc.psum_pool(name="ps_m", bufs=3))
             ps_s = ph2.enter_context(tc.psum_pool(name="ps_s", bufs=5))
             o_pool = ph2.enter_context(tc.tile_pool(name="o_pool", bufs=4))
+            l_pool = ph2.enter_context(tc.tile_pool(name="l_pool", bufs=3))
             g0 = 0
             for ng in OUT_BLOCKS:
                 w = ng * P
@@ -261,6 +292,7 @@ def tile_mixture_t_kernel(tc, inputs, biases, out):
                 bcast(g0, 0, ng, mb_v)
                 for ft in range(2):
                     o_t = o_pool.tile([P, BLK], F32, tag="o%d" % ft)
+                    l_t = l_pool.tile([P, BLK], F32, tag="l%d" % ft)
                     for c0 in range(0, w, 512):
                         cw = min(512, w - c0)
                         cols = slice(px + c0, px + c0 + cw)
@@ -274,7 +306,12 @@ def tile_mixture_t_kernel(tc, inputs, biases, out):
                             start=True,
                             stop=True,
                         )
-                        nc.scalar.activation(out=o_t[:, c0 : c0 + cw], in_=s[:, 0:cw], func=ACT.Ln)
-                    nc.vector.tensor_tensor(out=o_t[:, 0:w], in0=o_t[:, 0:w], in1=mb_v[:, 0:w], op=ALU.subtract)
+                        nc.scalar.activation(out=l_t[:, c0 : c0 + cw], in_=s[:, 0:cw], func=ACT.Ln)
+                    nc.vector.tensor_tensor(
+                        out=o_t[:, 0:w].rearrange("p (g q e) -> p g q e", q=P, e=2),
+                        in0=l_t[:, 0:w].rearrange("p (g e q) -> p g q e", q=P, e=2),
+                        in1=mb_v[:, 0:w].rearrange("p (g e q) -> p g q e", q=P, e=2),
+                        op=ALU.subtract,
+                    )
                     nc.sync.dma_start(out=o[px // HW, ft, :, px % HW : px % HW + w], in_=o_t[:, 0:w])
                 g0 += ng

@@ -25,10 +25,11 @@ FLOPS = 2 * B * HW * C * F
 def tile_mixture_t_kernel(tc, inputs, biases, out):
     nc = tc.nc
     BLOCKS = (
-        [(2, 2, 0), (2, 0, 0), (4, 2, 0)]
-        + [(8, 4, 1), (8, 2, 2)] * 6
-        + [(8, 2, 2), (8, 2, 1)]
-        + [(4, 0, 2), (4, 0, 1)]
+        [(2, 1, 0), (2, 1, 0), (4, 2, 0)]
+        + [(8, 3, 2)] * 4
+        + [(8, 4, 1), (8, 3, 1)] * 3
+        + [(8, 3, 2)] * 4
+        + [(4, 1, 1), (4, 0, 1)]
     )
     OUT_BLOCKS = [8] * 15 + [4, 2, 2]
     x = inputs.rearrange("b (p j) h w -> b p j (h w)", j=J)
@@ -119,11 +120,7 @@ def tile_mixture_t_kernel(tc, inputs, biases, out):
                     ng = BLOCKS[k1][0]
                     g0 = g0_of[k1]
                     nc.vector.tensor_reduce(
-                        out=nm32[:, g0 : g0 + ng].rearrange("q (g e) -> q g e", e=2),
-                        in_=xmt_of[k1][:].bitcast(BF16).rearrange("q (g p e) -> q g e p", p=P, e=2)[:, 0 : ng // 2, :, :],
-                        axis=AX.X,
-                        op=ALU.max,
-                        negate=True,
+                        out=nm32[:, g0 : g0 + ng], in_=xmt_of[k1][:, 0:ng, :], axis=AX.X, op=ALU.max, negate=True
                     )
                     nc.gpsimd.tensor_copy(out=nm16[:, g0 : g0 + ng], in_=nm32[:, g0 : g0 + ng])
                 if it < nb:
@@ -136,11 +133,9 @@ def tile_mixture_t_kernel(tc, inputs, biases, out):
                         out=a2[:, :, 0:w], in0=t_in[:, 0:2, 0:w], in1=t_in[:, 2:4, 0:w], op=ALU.max
                     )
                     nc.vector.tensor_tensor(out=xm[:, 0:w], in0=a2[:, 0, 0:w], in1=a2[:, 1, 0:w], op=ALU.max)
-                    xmt = ps_x.tile([P, 512], F32)
-                    for i in range(ng // 2):
-                        nc.tensor.transpose(
-                            xmt[:, i * P : (i + 1) * P], xm[:].bitcast(F32)[:, i * P : (i + 1) * P], ident32[:]
-                        )
+                    xmt = ps_x.tile([P, SUB, P], BF16)
+                    for i in range(ng):
+                        nc.tensor.transpose(xmt[:, i, :], xm[:, i * P : (i + 1) * P], ident[:])
                     xmt_of[it] = xmt
                 if 0 <= k2 < nb:
                     nbg = BLOCKS[k2][1]
@@ -150,21 +145,20 @@ def tile_mixture_t_kernel(tc, inputs, biases, out):
                     for g in range(nbg):
                         nc.scalar.activation(
                             out=esb_of[k2][:, g, :],
-                            in_=xt_of[k2][g // 2][:].bitcast(BF16).rearrange("q (c e) -> q e c", e=2)[:, g % 2, :],
+                            in_=xt_of[k2][g // 2][:, g % 2, :],
                             func=ACT.Exp,
                             bias=nm32[:, g0_of[k2] + g : g0_of[k2] + g + 1],
                         )
                 if 0 <= k1 < nb:
                     nbg = BLOCKS[k1][1]
                     xt_of[k1] = []
-                    for t in range(nbg // 2):
-                        xt = ps_t.tile([P, C], F32)
-                        for j in range(J):
-                            nc.tensor.transpose(
-                                xt[:, j * P : (j + 1) * P],
-                                t_of[k1][:, j, :].bitcast(F32)[:, t * P : (t + 1) * P],
-                                ident32[:],
-                            )
+                    for t in range((nbg + 1) // 2):
+                        xt = ps_t.tile([P, 2, C], BF16)
+                        for g in range(2 * t, min(2 * t + 2, nbg)):
+                            for j in range(J):
+                                nc.tensor.transpose(
+                                    xt[:, g % 2, j * P : (j + 1) * P], t_of[k1][:, j, g * P : (g + 1) * P], ident[:]
+                                )
                         xt_of[k1].append(xt)
                 if 0 <= k3 < nb:
                     ng, nbg, nfg = BLOCKS[k3]
@@ -184,13 +178,8 @@ def tile_mixture_t_kernel(tc, inputs, biases, out):
                         g = nbg + f
                         col = g0_of[k2] + g
                         df = ps_f.tile([P, J, P], F32)
-                        pair = t_of[k2][:, :, (g // 2) * 256 : (g // 2 + 1) * 256]
                         nc.tensor.matmul(
-                            out=df[:],
-                            lhsT=ident[:],
-                            rhs=pair.rearrange("p j (q e) -> p j q e", e=2)[:, :, :, g % 2],
-                            start=True,
-                            stop=False,
+                            out=df[:], lhsT=ident[:], rhs=t_of[k2][:, :, g * P : (g + 1) * P], start=True, stop=False
                         )
                         for j in range(J):
                             nc.tensor.matmul(
@@ -206,47 +195,28 @@ def tile_mixture_t_kernel(tc, inputs, biases, out):
                     ng, nbg, nfg = BLOCKS[k3]
                     a0 = nbg + nfg
                     aw = (ng - a0) * P
-                    if aw > 0:
-                        nc.scalar.activation(
-                            out=grp_of[k3][:, a0 * P * J : ng * P * J],
-                            in_=dv_of[k3][:, 0:aw, :].rearrange("p w j -> p (w j)"),
-                            func=ACT.Exp,
-                        )
+                    nc.scalar.activation(
+                        out=grp_of[k3][:, a0 * P * J : ng * P * J],
+                        in_=dv_of[k3][:, 0:aw, :].rearrange("p w j -> p (w j)"),
+                        func=ACT.Exp,
+                    )
                 if 0 <= k2 < nb:
                     ng, nbg, nfg = BLOCKS[k2]
                     a0 = nbg + nfg
                     aw = (ng - a0) * P
-                    if aw > 0:
-                        d_v = d_pool.tile([P, 5 * P, J], F32)
-                        dv_of[k2] = d_v
-                    g = a0
-                    while g < ng:
-                        pair = t_of[k2][:, :, (g // 2) * 256 : (g // 2 + 1) * 256].rearrange("p j (q e) -> p e q j", e=2)
-                        if g % 2 == 1:
-                            nc.vector.tensor_tensor(
-                                out=d_v[:, (g - a0) * P : (g - a0 + 1) * P, :],
-                                in0=pair[:, 1, :, :],
-                                in1=mbv_of[k2][:, g * P : (g + 1) * P].unsqueeze(2).to_broadcast([P, P, J]),
-                                op=ALU.add,
-                            )
-                            g += 1
-                        else:
-                            nc.vector.tensor_tensor(
-                                out=d_v[:, (g - a0) * P : (g - a0 + 2) * P, :].rearrange("p (e q) j -> p e q j", e=2),
-                                in0=pair,
-                                in1=mbv_of[k2][:, g * P : (g + 2) * P]
-                                .rearrange("p (e q) -> p e q", e=2)
-                                .unsqueeze(3)
-                                .to_broadcast([P, 2, P, J]),
-                                op=ALU.add,
-                            )
-                            g += 2
+                    d_v = d_pool.tile([P, 4 * P, J], F32)
+                    nc.vector.tensor_tensor(
+                        out=d_v[:, 0:aw, :],
+                        in0=t_of[k2][:, :, a0 * P : ng * P].rearrange("p j w -> p w j"),
+                        in1=mbv_of[k2][:, a0 * P : ng * P].unsqueeze(2).to_broadcast([P, aw, J]),
+                        op=ALU.add,
+                    )
+                    dv_of[k2] = d_v
                 if 0 <= k1 < nb:
                     ng, nbg, nfg = BLOCKS[k1]
-                    if nbg + nfg < ng:
-                        mb_v = ps_v.tile([P, BLK], BF16)
-                        bcast(g0_of[k1], nbg + nfg, ng, mb_v)
-                        mbv_of[k1] = mb_v
+                    mb_v = ps_v.tile([P, BLK], BF16)
+                    bcast(g0_of[k1], nbg + nfg, ng, mb_v)
+                    mbv_of[k1] = mb_v
                 if it + 2 < nb:
                     load(it + 2)
                 if 0 <= k5 < nb:
@@ -283,7 +253,6 @@ def tile_mixture_t_kernel(tc, inputs, biases, out):
             ps_m = ph2.enter_context(tc.psum_pool(name="ps_m", bufs=3))
             ps_s = ph2.enter_context(tc.psum_pool(name="ps_s", bufs=5))
             o_pool = ph2.enter_context(tc.tile_pool(name="o_pool", bufs=4))
-            l_pool = ph2.enter_context(tc.tile_pool(name="l_pool", bufs=3))
             g0 = 0
             for ng in OUT_BLOCKS:
                 w = ng * P
@@ -292,7 +261,6 @@ def tile_mixture_t_kernel(tc, inputs, biases, out):
                 bcast(g0, 0, ng, mb_v)
                 for ft in range(2):
                     o_t = o_pool.tile([P, BLK], F32, tag="o%d" % ft)
-                    l_t = l_pool.tile([P, BLK], F32, tag="l%d" % ft)
                     for c0 in range(0, w, 512):
                         cw = min(512, w - c0)
                         cols = slice(px + c0, px + c0 + cw)
@@ -306,12 +274,7 @@ def tile_mixture_t_kernel(tc, inputs, biases, out):
                             start=True,
                             stop=True,
                         )
-                        nc.scalar.activation(out=l_t[:, c0 : c0 + cw], in_=s[:, 0:cw], func=ACT.Ln)
-                    nc.vector.tensor_tensor(
-                        out=o_t[:, 0:w].rearrange("p (g q e) -> p g q e", q=P, e=2),
-                        in0=l_t[:, 0:w].rearrange("p (g e q) -> p g q e", q=P, e=2),
-                        in1=mb_v[:, 0:w].rearrange("p (g e q) -> p g q e", q=P, e=2),
-                        op=ALU.subtract,
-                    )
+                        nc.scalar.activation(out=o_t[:, c0 : c0 + cw], in_=s[:, 0:cw], func=ACT.Ln)
+                    nc.vector.tensor_tensor(out=o_t[:, 0:w], in0=o_t[:, 0:w], in1=mb_v[:, 0:w], op=ALU.subtract)
                     nc.sync.dma_start(out=o[px // HW, ft, :, px % HW : px % HW + w], in_=o_t[:, 0:w])
                 g0 += ng

@@ -21,16 +21,12 @@ BLK = 1024
 SUB = BLK // P
 FLOPS = 2 * B * HW * C * F
 
+S_EVERY = 4
+
 
 def tile_mixture_t_kernel(tc, inputs, biases, out):
     nc = tc.nc
-    BLOCKS = (
-        [(2, 1, 0), (2, 1, 0), (4, 2, 0)]
-        + [(8, 3, 2)] * 4
-        + [(8, 4, 1), (8, 3, 1)] * 3
-        + [(8, 3, 2)] * 4
-        + [(4, 1, 1), (4, 0, 1)]
-    )
+    BLOCKS = [(2, 0), (2, 0), (4, 0)] + [(8, 2)] * 12 + [(8, 0)] * 2 + [(4, 0), (4, 0)]
     OUT_BLOCKS = [8] * 15 + [4, 2, 2]
     x = inputs.rearrange("b (p j) h w -> b p j (h w)", j=J)
     bia = biases[0, 0].rearrange("(p j) f -> p j f", j=J)
@@ -38,6 +34,30 @@ def tile_mixture_t_kernel(tc, inputs, biases, out):
     nb = len(BLOCKS)
     g0_of = [sum([b[0] for b in BLOCKS[:k]]) for k in range(nb)]
     assert g0_of[-1] + BLOCKS[-1][0] == NGRP and sum(OUT_BLOCKS) == NGRP
+
+    units = []
+    first_unit = []
+    last_unit = []
+    for k in range(nb):
+        ng, nf = BLOCKS[k]
+        nbg = ng - nf
+        b_units = [("B", g, min(2, nbg - g)) for g in range(0, nbg, 2)]
+        f_units = [("F", nbg + f, 1) for f in range(nf)]
+        mixed = []
+        for i in range(max(len(b_units), len(f_units))):
+            if i < len(b_units):
+                mixed.append(b_units[i])
+            if i < len(f_units):
+                mixed.append(f_units[i])
+        first_unit.append(len(units))
+        for i in range(len(mixed)):
+            units.append((k, mixed[i][0], mixed[i][1], mixed[i][2], i, len(mixed)))
+        last_unit.append(len(units) - 1)
+    nu = len(units)
+    b_rank = {}
+    for s in range(nu):
+        if units[s][1] == "B":
+            b_rank[s] = len(b_rank)
 
     with ExitStack() as ctx:
         ctx.enter_context(tc.manual_schedule())
@@ -70,17 +90,14 @@ def tile_mixture_t_kernel(tc, inputs, biases, out):
                 )
 
         with ExitStack() as ph1:
-            ps_v = ph1.enter_context(tc.psum_pool(name="ps_v", bufs=1))
             ps_x = ph1.enter_context(tc.psum_pool(name="ps_x", bufs=1))
-            ps_f = ph1.enter_context(tc.psum_pool(name="ps_f", bufs=2))
-            ps_t = ph1.enter_context(tc.psum_pool(name="ps_t", bufs=2))
-            ps_e = ph1.enter_context(tc.psum_pool(name="ps_e", bufs=2))
-            t_pool = ph1.enter_context(tc.tile_pool(name="t_pool", bufs=4))
+            ps_w = ph1.enter_context(tc.psum_pool(name="ps_w", bufs=4))
+            ps_e = ph1.enter_context(tc.psum_pool(name="ps_e", bufs=3))
+            t_pool = ph1.enter_context(tc.tile_pool(name="t_pool", bufs=5))
             w_pool = ph1.enter_context(tc.tile_pool(name="w_pool", bufs=2))
-            d_pool = ph1.enter_context(tc.tile_pool(name="d_pool", bufs=3))
             e_pool = ph1.enter_context(tc.tile_pool(name="e_pool", bufs=3))
             g_pool = ph1.enter_context(tc.tile_pool(name="g_pool", bufs=4))
-            t_of, xmt_of, mbv_of, xt_of, esb_of, et_of, grp_of, dv_of, df_of = {}, {}, {}, {}, {}, {}, {}, {}, {}
+            t_of, a2_of, xm_of, xmt_of, fw_of, esb_of, eb_of, grp_of = {}, {}, {}, {}, {}, {}, {}, {}
 
             def load(k):
                 t_in = t_pool.tile([P, J, BLK], BF16)
@@ -89,165 +106,175 @@ def tile_mixture_t_kernel(tc, inputs, biases, out):
                 nc.sync.dma_start(out=t_in[:, :, 0:w], in_=x[px // HW, :, :, px % HW : px % HW + w])
                 t_of[k] = t_in
 
+            def tree1(k):
+                w = BLOCKS[k][0] * P
+                a2 = w_pool.tile([P, 2, BLK], BF16)
+                nc.vector.tensor_tensor(
+                    out=a2[:, :, 0:w], in0=t_of[k][:, 0:2, 0:w], in1=t_of[k][:, 2:4, 0:w], op=ALU.max
+                )
+                a2_of[k] = a2
+
+            def tree2(k):
+                w = BLOCKS[k][0] * P
+                xm = w_pool.tile([P, BLK], BF16)
+                nc.vector.tensor_tensor(out=xm[:, 0:w], in0=a2_of[k][:, 0, 0:w], in1=a2_of[k][:, 1, 0:w], op=ALU.max)
+                xm_of[k] = xm
+
+            def turn_max(k):
+                xmt = ps_x.tile([P, SUB, P], BF16)
+                for i in range(BLOCKS[k][0]):
+                    nc.tensor.transpose(xmt[:, i, :], xm_of[k][:, i * P : (i + 1) * P], ident[:])
+                xmt_of[k] = xmt
+
+            def reduce_max(k):
+                ng = BLOCKS[k][0]
+                g0 = g0_of[k]
+                nc.vector.tensor_reduce(
+                    out=nm32[:, g0 : g0 + ng], in_=xmt_of[k][:, 0:ng, :], axis=AX.X, op=ALU.max, negate=True
+                )
+                nc.gpsimd.tensor_copy(out=nm16[:, g0 : g0 + ng], in_=nm32[:, g0 : g0 + ng])
+
+            def forward(s):
+                k, kind, g, n, i_in, n_in = units[s]
+                if i_in == 0:
+                    grp = g_pool.tile([P, BLK * J], BF16, align_bytes=64)
+                    grp_of[k] = grp
+                if kind == "B":
+                    xt = ps_w.tile([P, 2, J, P], BF16, tag="fw")
+                    for i in range(n):
+                        for j in range(J):
+                            nc.tensor.transpose(
+                                xt[:, i, j, :], t_of[k][:, j, (g + i) * P : (g + i + 1) * P], ident[:]
+                            )
+                    fw_of[s] = xt
+                else:
+                    col = g0_of[k] + g
+                    df = ps_w.tile([P, J, P], F32, tag="fw")
+                    nc.tensor.matmul(
+                        out=df[:], lhsT=ident[:], rhs=t_of[k][:, :, g * P : (g + 1) * P], start=True, stop=False
+                    )
+                    for j in range(J):
+                        nc.tensor.matmul(
+                            out=df[:, j, :],
+                            lhsT=nm32[:, col : col + 1].to_broadcast([P, P]),
+                            rhs=ident32[:],
+                            is_transpose=True,
+                            start=False,
+                            stop=(j == J - 1),
+                        )
+                    fw_of[s] = df
+
+            def exponent(s):
+                k, kind, g, n, i_in, n_in = units[s]
+                if kind == "B":
+                    e_sb = e_pool.tile([P, 2, C], BF16)
+                    for i in range(n):
+                        col = g0_of[k] + g + i
+                        nc.scalar.activation(
+                            out=e_sb[:, i, :].rearrange("q (u p t) -> q u p t", u=2, t=2),
+                            in_=fw_of[s][:, i, :, :].rearrange("q (u t) p -> q u p t", t=2),
+                            func=ACT.Exp,
+                            bias=nm32[:, col : col + 1],
+                        )
+                    esb_of[s] = e_sb
+                else:
+                    nc.scalar.activation(
+                        out=grp_of[k][:, g * 512 : (g + 1) * 512].rearrange("p (w j) -> p w j", j=J),
+                        in_=fw_of[s][:].rearrange("p j w -> p w j"),
+                        func=ACT.Exp,
+                    )
+
+            def backward(s):
+                k, kind, g, n, i_in, n_in = units[s]
+                if kind == "B":
+                    eb = ps_e.tile([P, 2, 2, P], F32)
+                    for i in range(n):
+                        words = esb_of[s][:, i, :].bitcast(F32)
+                        for u in range(2):
+                            nc.tensor.transpose(eb[:, i, u, :], words[:, u * P : (u + 1) * P], ident32[:])
+                    eb_of[s] = eb
+
+            def copy_out(s):
+                k, kind, g, n, i_in, n_in = units[s]
+                if kind == "B":
+                    dst = grp_of[k][:, g * 512 : (g + n) * 512].bitcast(F32).rearrange("p (i w u) -> p i w u", i=n, u=2)
+                    src = eb_of[s][:, 0:n, :, :].rearrange("p i u w -> p i w u")
+                    if b_rank[s] % S_EVERY == S_EVERY - 1:
+                        nc.scalar.copy(out=dst, in_=src)
+                    else:
+                        nc.vector.tensor_copy(out=dst, in_=src)
+
+            def quantise(k):
+                c0 = g0_of[k] * P
+                w = BLOCKS[k][0] * P
+                nc.vector.quantize_mx(
+                    out=codes[:, c0 : c0 + w].bitcast(FP8X4),
+                    scales=scales[:, c0 : c0 + w],
+                    in_=grp_of[k][:, 0 : w * J],
+                )
+
             load(0)
             load(1)
             nc.sync.dma_start(out=b_raw[:], in_=bia)
+            load(2)
+            load(3)
 
-            for it in range(nb + 5):
-                k1, k2, k3, k4, k5 = it - 1, it - 2, it - 3, it - 4, it - 5
-                if 0 <= k4 < nb:
-                    nbg = BLOCKS[k4][1]
-                    for t in range((nbg + 1) // 2):
-                        n = min(2, nbg - 2 * t)
-                        nc.scalar.copy(
-                            out=grp_of[k4][:, t * 1024 : t * 1024 + n * 512].rearrange(
-                                "p (g w j) -> p g w j", g=n, j=J
-                            ),
-                            in_=et_of[k4][t][:, 0:n, :, :].rearrange("p g j w -> p g w j"),
+            for s in range(nu + 6):
+                if 0 <= s - 2 < nu:
+                    backward(s - 2)
+                if s < nu:
+                    forward(s)
+                if s == 0:
+                    tree1(0)
+                    tree2(0)
+                    turn_max(0)
+                    tree1(1)
+                    tree2(1)
+                    reduce_max(0)
+                    turn_max(1)
+                    reduce_max(1)
+                if 0 <= s - 1 < nu:
+                    exponent(s - 1)
+                if 0 <= s - 3 < nu:
+                    copy_out(s - 3)
+                if s < nu:
+                    k, kind, g, n, i_in, n_in = units[s]
+                    k2 = k + 2
+                    if i_in == 0 and k + 4 < nb:
+                        load(k + 4)
+                    if k2 < nb:
+                        if i_in == 0:
+                            tree1(k2)
+                        if i_in == min(1, n_in - 1):
+                            tree2(k2)
+                        if i_in == min(2, n_in - 1):
+                            turn_max(k2)
+                        if i_in == min(3, n_in - 1):
+                            reduce_max(k2)
+                    if k == 4 and i_in == 0:
+                        nc.scalar.activation(out=sq[:], in_=b_raw[:], func=ACT.Square)
+                        nc.gpsimd.tensor_tensor(out=js1[:], in0=sq[:, 0:2, :], in1=sq[:, 2:4, :], op=ALU.add)
+                        nc.gpsimd.tensor_tensor(out=js[:], in0=js1[:, 0, :], in1=js1[:, 1, :], op=ALU.add)
+                    if k == 6 and i_in == n_in - 1:
+                        col_sum = ps_x.tile([P, 512], F32, tag="xmt")
+                        nc.tensor.matmul(out=col_sum[:, 0:F], lhsT=ones[:], rhs=js[:], start=True, stop=True)
+                    if k == 7 and i_in == 0:
+                        nc.vector.reciprocal(out=rs[:], in_=col_sum[:, 0:F])
+                        nc.gpsimd.tensor_tensor(
+                            out=p_grp[:],
+                            in0=sq[:].rearrange("p j f -> p f j"),
+                            in1=rs[:].unsqueeze(2).to_broadcast([P, F, J]),
+                            op=ALU.mult,
                         )
-                if 0 <= k3 < nb:
-                    nbg = BLOCKS[k3][1]
-                    et_of[k3] = []
-                    for t in range((nbg + 1) // 2):
-                        et = ps_e.tile([P, 2, J, P], BF16)
-                        for g in range(2 * t, min(2 * t + 2, nbg)):
-                            for j in range(J):
-                                nc.tensor.transpose(
-                                    et[:, g % 2, j, :], esb_of[k3][:, g, j * P : (j + 1) * P], ident[:]
-                                )
-                        et_of[k3].append(et)
-                if 0 <= k1 < nb:
-                    ng = BLOCKS[k1][0]
-                    g0 = g0_of[k1]
-                    nc.vector.tensor_reduce(
-                        out=nm32[:, g0 : g0 + ng], in_=xmt_of[k1][:, 0:ng, :], axis=AX.X, op=ALU.max, negate=True
-                    )
-                    nc.gpsimd.tensor_copy(out=nm16[:, g0 : g0 + ng], in_=nm32[:, g0 : g0 + ng])
-                if it < nb:
-                    ng = BLOCKS[it][0]
-                    w = ng * P
-                    t_in = t_of[it]
-                    a2 = w_pool.tile([P, 2, BLK], BF16)
-                    xm = w_pool.tile([P, BLK], BF16)
-                    nc.vector.tensor_tensor(
-                        out=a2[:, :, 0:w], in0=t_in[:, 0:2, 0:w], in1=t_in[:, 2:4, 0:w], op=ALU.max
-                    )
-                    nc.vector.tensor_tensor(out=xm[:, 0:w], in0=a2[:, 0, 0:w], in1=a2[:, 1, 0:w], op=ALU.max)
-                    xmt = ps_x.tile([P, SUB, P], BF16)
-                    for i in range(ng):
-                        nc.tensor.transpose(xmt[:, i, :], xm[:, i * P : (i + 1) * P], ident[:])
-                    xmt_of[it] = xmt
-                if 0 <= k2 < nb:
-                    nbg = BLOCKS[k2][1]
-                    if nbg > 0:
-                        e_sb = e_pool.tile([P, 4, C], BF16)
-                        esb_of[k2] = e_sb
-                    for g in range(nbg):
-                        nc.scalar.activation(
-                            out=esb_of[k2][:, g, :],
-                            in_=xt_of[k2][g // 2][:, g % 2, :],
-                            func=ACT.Exp,
-                            bias=nm32[:, g0_of[k2] + g : g0_of[k2] + g + 1],
+                    if k == 9 and i_in == 1:
+                        nc.vector.quantize_mx(
+                            out=p_codes[:].bitcast(FP8X4),
+                            scales=p_scales[:],
+                            in_=p_grp[:].rearrange("p f j -> p (f j)"),
                         )
-                if 0 <= k1 < nb:
-                    nbg = BLOCKS[k1][1]
-                    xt_of[k1] = []
-                    for t in range((nbg + 1) // 2):
-                        xt = ps_t.tile([P, 2, C], BF16)
-                        for g in range(2 * t, min(2 * t + 2, nbg)):
-                            for j in range(J):
-                                nc.tensor.transpose(
-                                    xt[:, g % 2, j * P : (j + 1) * P], t_of[k1][:, j, g * P : (g + 1) * P], ident[:]
-                                )
-                        xt_of[k1].append(xt)
-                if 0 <= k3 < nb:
-                    ng, nbg, nfg = BLOCKS[k3]
-                    grp = g_pool.tile([P, BLK * J], BF16, align_bytes=64)
-                    grp_of[k3] = grp
-                    for f in range(nfg):
-                        g = nbg + f
-                        nc.scalar.activation(
-                            out=grp[:, g * 512 : (g + 1) * 512].rearrange("p (w j) -> p w j", j=J),
-                            in_=df_of[k3][f][:].rearrange("p j w -> p w j"),
-                            func=ACT.Exp,
-                        )
-                if 0 <= k2 < nb:
-                    ng, nbg, nfg = BLOCKS[k2]
-                    df_of[k2] = []
-                    for f in range(nfg):
-                        g = nbg + f
-                        col = g0_of[k2] + g
-                        df = ps_f.tile([P, J, P], F32)
-                        nc.tensor.matmul(
-                            out=df[:], lhsT=ident[:], rhs=t_of[k2][:, :, g * P : (g + 1) * P], start=True, stop=False
-                        )
-                        for j in range(J):
-                            nc.tensor.matmul(
-                                out=df[:, j, :],
-                                lhsT=nm32[:, col : col + 1].to_broadcast([P, P]),
-                                rhs=ident32[:],
-                                is_transpose=True,
-                                start=False,
-                                stop=(j == J - 1),
-                            )
-                        df_of[k2].append(df)
-                if 0 <= k3 < nb:
-                    ng, nbg, nfg = BLOCKS[k3]
-                    a0 = nbg + nfg
-                    aw = (ng - a0) * P
-                    nc.scalar.activation(
-                        out=grp_of[k3][:, a0 * P * J : ng * P * J],
-                        in_=dv_of[k3][:, 0:aw, :].rearrange("p w j -> p (w j)"),
-                        func=ACT.Exp,
-                    )
-                if 0 <= k2 < nb:
-                    ng, nbg, nfg = BLOCKS[k2]
-                    a0 = nbg + nfg
-                    aw = (ng - a0) * P
-                    d_v = d_pool.tile([P, 4 * P, J], F32)
-                    nc.vector.tensor_tensor(
-                        out=d_v[:, 0:aw, :],
-                        in0=t_of[k2][:, :, a0 * P : ng * P].rearrange("p j w -> p w j"),
-                        in1=mbv_of[k2][:, a0 * P : ng * P].unsqueeze(2).to_broadcast([P, aw, J]),
-                        op=ALU.add,
-                    )
-                    dv_of[k2] = d_v
-                if 0 <= k1 < nb:
-                    ng, nbg, nfg = BLOCKS[k1]
-                    mb_v = ps_v.tile([P, BLK], BF16)
-                    bcast(g0_of[k1], nbg + nfg, ng, mb_v)
-                    mbv_of[k1] = mb_v
-                if it + 2 < nb:
-                    load(it + 2)
-                if 0 <= k5 < nb:
-                    c0 = g0_of[k5] * P
-                    w = BLOCKS[k5][0] * P
-                    nc.vector.quantize_mx(
-                        out=codes[:, c0 : c0 + w].bitcast(FP8X4),
-                        scales=scales[:, c0 : c0 + w],
-                        in_=grp_of[k5][:, 0 : w * J],
-                    )
-                if it == 5:
-                    nc.scalar.activation(out=sq[:], in_=b_raw[:], func=ACT.Square)
-                    nc.gpsimd.tensor_tensor(out=js1[:], in0=sq[:, 0:2, :], in1=sq[:, 2:4, :], op=ALU.add)
-                    nc.gpsimd.tensor_tensor(out=js[:], in0=js1[:, 0, :], in1=js1[:, 1, :], op=ALU.add)
-                if it == nb:
-                    col_sum = ps_x.tile([P, 512], F32, tag="xmt")
-                    nc.tensor.matmul(out=col_sum[:, 0:F], lhsT=ones[:], rhs=js[:], start=True, stop=True)
-                if it == nb + 1:
-                    nc.vector.reciprocal(out=rs[:], in_=col_sum[:, 0:F])
-                    nc.gpsimd.tensor_tensor(
-                        out=p_grp[:],
-                        in0=sq[:].rearrange("p j f -> p f j"),
-                        in1=rs[:].unsqueeze(2).to_broadcast([P, F, J]),
-                        op=ALU.mult,
-                    )
-                if it == nb + 2:
-                    nc.vector.quantize_mx(
-                        out=p_codes[:].bitcast(FP8X4),
-                        scales=p_scales[:],
-                        in_=p_grp[:].rearrange("p f j -> p (f j)"),
-                    )
+                for k in range(nb):
+                    if last_unit[k] + 5 == s:
+                        quantise(k)
 
         with ExitStack() as ph2:
             ps_m = ph2.enter_context(tc.psum_pool(name="ps_m", bufs=3))
@@ -264,9 +291,9 @@ def tile_mixture_t_kernel(tc, inputs, biases, out):
                     for c0 in range(0, w, 512):
                         cw = min(512, w - c0)
                         cols = slice(px + c0, px + c0 + cw)
-                        s = ps_s.tile([P, 512], F32)
+                        s_ps = ps_s.tile([P, 512], F32)
                         nc.tensor.matmul_mx(
-                            out=s[:, 0:cw],
+                            out=s_ps[:, 0:cw],
                             lhsT=p_codes[:, ft * P : (ft + 1) * P].bitcast(FP8X4),
                             lhsT_scale=p_scales[:, ft * P : (ft + 1) * P],
                             rhs=codes[:, cols].bitcast(FP8X4),
@@ -274,7 +301,7 @@ def tile_mixture_t_kernel(tc, inputs, biases, out):
                             start=True,
                             stop=True,
                         )
-                        nc.scalar.activation(out=o_t[:, c0 : c0 + cw], in_=s[:, 0:cw], func=ACT.Ln)
+                        nc.scalar.activation(out=o_t[:, c0 : c0 + cw], in_=s_ps[:, 0:cw], func=ACT.Ln)
                     nc.vector.tensor_tensor(out=o_t[:, 0:w], in0=o_t[:, 0:w], in1=mb_v[:, 0:w], op=ALU.subtract)
                     nc.sync.dma_start(out=o[px // HW, ft, :, px % HW : px % HW + w], in_=o_t[:, 0:w])
                 g0 += ng

@@ -21,12 +21,13 @@ BLK = 1024
 SUB = BLK // P
 FLOPS = 2 * B * HW * C * F
 
-S_EVERY = 4
+WARM_N = 192
+S_EVERY = 3
 
 
 def tile_mixture_t_kernel(tc, inputs, biases, out):
     nc = tc.nc
-    BLOCKS = [(2, 0), (2, 0), (4, 0)] + [(8, 2)] * 12 + [(8, 0)] * 2 + [(4, 0), (4, 0)]
+    BLOCKS = [(2, 0), (2, 0), (4, 0)] + [(8, 0)] * 14 + [(4, 0), (4, 0)]
     OUT_BLOCKS = [8] * 15 + [4, 2, 2]
     x = inputs.rearrange("b (p j) h w -> b p j (h w)", j=J)
     bia = biases[0, 0].rearrange("(p j) f -> p j f", j=J)
@@ -78,10 +79,12 @@ def tile_mixture_t_kernel(tc, inputs, biases, out):
         p_grp = keep.tile([P, F, J], BF16, align_bytes=64)
         p_codes = keep.tile([P, F], U32, align_bytes=64)
         p_scales = keep.tile([P, F], U8, align_bytes=64)
+        warm_rhs = keep.tile([P, WARM_N], F32)
 
         make_identity(nc, ident[:])
         make_identity(nc, ident32[:])
         nc.gpsimd.memset(ones[:], 1.0)
+        nc.gpsimd.memset(warm_rhs[:], 1.0)
 
         def bcast(g0, first, last, mb_v):
             for i in range(first, last):
@@ -91,7 +94,8 @@ def tile_mixture_t_kernel(tc, inputs, biases, out):
 
         with ExitStack() as ph1:
             ps_x = ph1.enter_context(tc.psum_pool(name="ps_x", bufs=1))
-            ps_w = ph1.enter_context(tc.psum_pool(name="ps_w", bufs=4))
+            ps_w = ph1.enter_context(tc.psum_pool(name="ps_w", bufs=3))
+            ps_d = ph1.enter_context(tc.psum_pool(name="ps_d", bufs=1))
             ps_e = ph1.enter_context(tc.psum_pool(name="ps_e", bufs=3))
             t_pool = ph1.enter_context(tc.tile_pool(name="t_pool", bufs=5))
             w_pool = ph1.enter_context(tc.tile_pool(name="w_pool", bufs=2))
@@ -213,15 +217,25 @@ def tile_mixture_t_kernel(tc, inputs, biases, out):
                     in_=grp_of[k][:, 0 : w * J],
                 )
 
+            warm_ps = ps_d.tile([P, 512], F32)
+
+            def warm(n):
+                nc.tensor.matmul(out=warm_ps[:, 0:n], lhsT=ones[:], rhs=warm_rhs[:, 0:n], start=True, stop=True)
+
             load(0)
             load(1)
             nc.sync.dma_start(out=b_raw[:], in_=bia)
             load(2)
             load(3)
 
+            for i in range(4):
+                warm(P)
+
             for s in range(nu + 6):
                 if 0 <= s - 2 < nu:
                     backward(s - 2)
+                if s < nu:
+                    warm(WARM_N)
                 if s < nu:
                     forward(s)
                 if s == 0:

@@ -86,10 +86,12 @@ def tile_mixture_t_kernel(tc, inputs, biases, out):
         nc.gpsimd.memset(ones[:], 1.0)
         nc.gpsimd.memset(warm_rhs[:], 1.0)
 
-        def bcast(g0, first, last, mb_v):
-            for i in range(first, last):
+        def bcast(g0, spans, mb_v):
+            for n in range(spans):
                 nc.tensor.transpose(
-                    mb_v[:, i * P : (i + 1) * P], nm16[:, g0 + i : g0 + i + 1].to_broadcast([P, P]), ident[:]
+                    mb_v[:, n * P : (n + 1) * P],
+                    nm16[:, g0 + 2 * n : g0 + 2 * n + 2].bitcast(F32).to_broadcast([P, P]),
+                    ident32[:],
                 )
 
         with ExitStack() as ph1:
@@ -125,16 +127,21 @@ def tile_mixture_t_kernel(tc, inputs, biases, out):
                 xm_of[k] = xm
 
             def turn_max(k):
-                xmt = ps_x.tile([P, SUB, P], BF16)
-                for i in range(BLOCKS[k][0]):
-                    nc.tensor.transpose(xmt[:, i, :], xm_of[k][:, i * P : (i + 1) * P], ident[:])
+                xmt = ps_x.tile([P, SUB // 2, P], F32)
+                words = xm_of[k][:].bitcast(F32)
+                for n in range(BLOCKS[k][0] // 2):
+                    nc.tensor.transpose(xmt[:, n, :], words[:, n * P : (n + 1) * P], ident32[:])
                 xmt_of[k] = xmt
 
             def reduce_max(k):
                 ng = BLOCKS[k][0]
                 g0 = g0_of[k]
                 nc.vector.tensor_reduce(
-                    out=nm32[:, g0 : g0 + ng], in_=xmt_of[k][:, 0:ng, :], axis=AX.X, op=ALU.max, negate=True
+                    out=nm32[:, g0 : g0 + ng].rearrange("q (n e) -> q n e", e=2),
+                    in_=xmt_of[k][:, 0 : ng // 2, :].bitcast(BF16).rearrange("q n (c e) -> q n e c", e=2),
+                    axis=AX.X,
+                    op=ALU.max,
+                    negate=True,
                 )
                 nc.gpsimd.tensor_copy(out=nm16[:, g0 : g0 + ng], in_=nm32[:, g0 : g0 + ng])
 
@@ -144,12 +151,11 @@ def tile_mixture_t_kernel(tc, inputs, biases, out):
                     grp = g_pool.tile([P, BLK * J], BF16, align_bytes=64)
                     grp_of[k] = grp
                 if kind == "B":
-                    xt = ps_w.tile([P, 2, J, P], BF16, tag="fw")
-                    for i in range(n):
-                        for j in range(J):
-                            nc.tensor.transpose(
-                                xt[:, i, j, :], t_of[k][:, j, (g + i) * P : (g + i + 1) * P], ident[:]
-                            )
+                    xt = ps_w.tile([P, J, P], F32, tag="fw")
+                    for j in range(J):
+                        nc.tensor.transpose(
+                            xt[:, j, :], t_of[k][:, j, g * P : (g + 2) * P].bitcast(F32), ident32[:]
+                        )
                     fw_of[s] = xt
                 else:
                     col = g0_of[k] + g
@@ -172,11 +178,12 @@ def tile_mixture_t_kernel(tc, inputs, biases, out):
                 k, kind, g, n, i_in, n_in = units[s]
                 if kind == "B":
                     e_sb = e_pool.tile([P, 2, C], BF16)
+                    halves = fw_of[s][:].bitcast(BF16).rearrange("q (u t) (p e) -> q e u p t", t=2, e=2)
                     for i in range(n):
                         col = g0_of[k] + g + i
                         nc.scalar.activation(
                             out=e_sb[:, i, :].rearrange("q (u p t) -> q u p t", u=2, t=2),
-                            in_=fw_of[s][:, i, :, :].rearrange("q (u t) p -> q u p t", t=2),
+                            in_=halves[:, i],
                             func=ACT.Exp,
                             bias=nm32[:, col : col + 1],
                         )
@@ -201,8 +208,8 @@ def tile_mixture_t_kernel(tc, inputs, biases, out):
             def copy_out(s):
                 k, kind, g, n, i_in, n_in = units[s]
                 if kind == "B":
-                    dst = grp_of[k][:, g * 512 : (g + n) * 512].bitcast(F32).rearrange("p (i w u) -> p i w u", i=n, u=2)
-                    src = eb_of[s][:, 0:n, :, :].rearrange("p i u w -> p i w u")
+                    dst = grp_of[k][:, g * 512 : (g + n) * 512].bitcast(F32).rearrange("p (q i u) -> p q i u", i=n, u=2)
+                    src = eb_of[s][:, 0:n, :, :].rearrange("p i u q -> p q i u")
                     if b_rank[s] % S_EVERY == S_EVERY - 1:
                         nc.scalar.copy(out=dst, in_=src)
                     else:
@@ -298,8 +305,8 @@ def tile_mixture_t_kernel(tc, inputs, biases, out):
             for ng in OUT_BLOCKS:
                 w = ng * P
                 px = g0 * P
-                mb_v = ps_m.tile([P, BLK], BF16)
-                bcast(g0, 0, ng, mb_v)
+                mb_v = ps_m.tile([P, BLK // 2], F32)
+                bcast(g0, ng // 2, mb_v)
                 for ft in range(2):
                     o_t = o_pool.tile([P, BLK], F32, tag="o%d" % ft)
                     for c0 in range(0, w, 512):
@@ -316,6 +323,6 @@ def tile_mixture_t_kernel(tc, inputs, biases, out):
                             stop=True,
                         )
                         nc.scalar.activation(out=o_t[:, c0 : c0 + cw], in_=s_ps[:, 0:cw], func=ACT.Ln)
-                    nc.vector.tensor_tensor(out=o_t[:, 0:w], in0=o_t[:, 0:w], in1=mb_v[:, 0:w], op=ALU.subtract)
+                    nc.vector.tensor_tensor(out=o_t[:, 0:w], in0=o_t[:, 0:w], in1=mb_v[:, 0 : w // 2].bitcast(BF16), op=ALU.subtract)
                     nc.sync.dma_start(out=o[px // HW, ft, :, px % HW : px % HW + w], in_=o_t[:, 0:w])
                 g0 += ng

@@ -238,14 +238,14 @@ def tile_mixture_t_kernel(tc, inputs, biases, out):
             for i in range(4):
                 warm(P)
 
-            for s in range(nu + 6):
+            for s in range(-1, nu + 6):
                 if 0 <= s - 2 < nu:
                     backward(s - 2)
-                if s < nu:
+                if 0 <= s < nu:
                     warm(WARM_N)
-                if s < nu:
-                    forward(s)
-                if s == 0:
+                if s + 1 < nu:
+                    forward(s + 1)
+                if s == -1:
                     tree1(0)
                     tree2(0)
                     turn_max(0)
@@ -258,27 +258,11 @@ def tile_mixture_t_kernel(tc, inputs, biases, out):
                     exponent(s - 1)
                 if 0 <= s - 3 < nu:
                     copy_out(s - 3)
-                if s < nu:
+                if 0 <= s < nu:
                     k, kind, g, n, i_in, n_in = units[s]
                     k2 = k + 2
                     if i_in == 0 and k + 4 < nb:
                         load(k + 4)
-                    if k2 < nb:
-                        if i_in == 0:
-                            tree1(k2)
-                        if i_in == min(1, n_in - 1):
-                            tree2(k2)
-                        if i_in == min(2, n_in - 1):
-                            turn_max(k2)
-                        if i_in == min(3, n_in - 1):
-                            reduce_max(k2)
-                    if k == 4 and i_in == 0:
-                        nc.scalar.activation(out=sq[:], in_=b_raw[:], func=ACT.Square)
-                        nc.gpsimd.tensor_tensor(out=js1[:], in0=sq[:, 0:2, :], in1=sq[:, 2:4, :], op=ALU.add)
-                        nc.gpsimd.tensor_tensor(out=js[:], in0=js1[:, 0, :], in1=js1[:, 1, :], op=ALU.add)
-                    if k == 6 and i_in == n_in - 1:
-                        col_sum = ps_x.tile([P, 512], F32, tag="xmt")
-                        nc.tensor.matmul(out=col_sum[:, 0:F], lhsT=ones[:], rhs=js[:], start=True, stop=True)
                     if k == 7 and i_in == 0:
                         nc.vector.reciprocal(out=rs[:], in_=col_sum[:, 0:F])
                         nc.gpsimd.tensor_tensor(
@@ -287,6 +271,22 @@ def tile_mixture_t_kernel(tc, inputs, biases, out):
                             in1=rs[:].unsqueeze(2).to_broadcast([P, F, J]),
                             op=ALU.mult,
                         )
+                    if 2 <= k + 1 < nb and i_in == min(1, n_in - 1):
+                        reduce_max(k + 1)
+                    if k2 < nb:
+                        if i_in == 0:
+                            tree1(k2)
+                        if i_in == min(1, n_in - 1):
+                            tree2(k2)
+                        if i_in == n_in - 1:
+                            turn_max(k2)
+                    if k == 4 and i_in == 0:
+                        nc.scalar.activation(out=sq[:], in_=b_raw[:], func=ACT.Square)
+                        nc.gpsimd.tensor_tensor(out=js1[:], in0=sq[:, 0:2, :], in1=sq[:, 2:4, :], op=ALU.add)
+                        nc.gpsimd.tensor_tensor(out=js[:], in0=js1[:, 0, :], in1=js1[:, 1, :], op=ALU.add)
+                    if k == 6 and i_in == n_in - 1:
+                        col_sum = ps_e.tile([P, 512], F32, tag="eb")
+                        nc.tensor.matmul(out=col_sum[:, 0:F], lhsT=ones[:], rhs=js[:], start=True, stop=True)
                     if k == 9 and i_in == 1:
                         nc.vector.quantize_mx(
                             out=p_codes[:].bitcast(FP8X4),

@@ -21,13 +21,12 @@ BLK = 1024
 SUB = BLK // P
 FLOPS = 2 * B * HW * C * F
 
-WARM_N = 192
 S_EVERY = 3
 
 
 def tile_mixture_t_kernel(tc, inputs, biases, out):
     nc = tc.nc
-    BLOCKS = [(2, 0), (2, 0), (4, 0)] + [(8, 0)] * 14 + [(4, 0), (4, 0)]
+    BLOCKS = [(2, 0), (2, 0), (4, 0)] + [(8, 2)] * 12 + [(8, 0)] * 2 + [(4, 0), (4, 0)]
     OUT_BLOCKS = [8] * 15 + [4, 2, 2]
     x = inputs.rearrange("b (p j) h w -> b p j (h w)", j=J)
     bia = biases[0, 0].rearrange("(p j) f -> p j f", j=J)
@@ -55,6 +54,9 @@ def tile_mixture_t_kernel(tc, inputs, biases, out):
             units.append((k, mixed[i][0], mixed[i][1], mixed[i][2], i, len(mixed)))
         last_unit.append(len(units) - 1)
     nu = len(units)
+    natural = []
+    for k in range(nb):
+        natural.extend([False] * (BLOCKS[k][0] - BLOCKS[k][1]) + [True] * BLOCKS[k][1])
     b_rank = {}
     for s in range(nu):
         if units[s][1] == "B":
@@ -79,25 +81,30 @@ def tile_mixture_t_kernel(tc, inputs, biases, out):
         p_grp = keep.tile([P, F, J], BF16, align_bytes=64)
         p_codes = keep.tile([P, F], U32, align_bytes=64)
         p_scales = keep.tile([P, F], U8, align_bytes=64)
-        warm_rhs = keep.tile([P, WARM_N], F32)
 
         make_identity(nc, ident[:])
         make_identity(nc, ident32[:])
         nc.gpsimd.memset(ones[:], 1.0)
-        nc.gpsimd.memset(warm_rhs[:], 1.0)
 
         def bcast(g0, spans, mb_v):
             for n in range(spans):
-                nc.tensor.transpose(
-                    mb_v[:, n * P : (n + 1) * P],
-                    nm16[:, g0 + 2 * n : g0 + 2 * n + 2].bitcast(F32).to_broadcast([P, P]),
-                    ident32[:],
-                )
+                if natural[g0 + 2 * n]:
+                    for i in range(2):
+                        nc.tensor.transpose(
+                            mb_v[:, n * P : (n + 1) * P].bitcast(BF16)[:, i * P : (i + 1) * P],
+                            nm16[:, g0 + 2 * n + i : g0 + 2 * n + i + 1].to_broadcast([P, P]),
+                            ident[:],
+                        )
+                else:
+                    nc.tensor.transpose(
+                        mb_v[:, n * P : (n + 1) * P],
+                        nm16[:, g0 + 2 * n : g0 + 2 * n + 2].bitcast(F32).to_broadcast([P, P]),
+                        ident32[:],
+                    )
 
         with ExitStack() as ph1:
             ps_x = ph1.enter_context(tc.psum_pool(name="ps_x", bufs=1))
-            ps_w = ph1.enter_context(tc.psum_pool(name="ps_w", bufs=3))
-            ps_d = ph1.enter_context(tc.psum_pool(name="ps_d", bufs=1))
+            ps_w = ph1.enter_context(tc.psum_pool(name="ps_w", bufs=4))
             ps_e = ph1.enter_context(tc.psum_pool(name="ps_e", bufs=3))
             t_pool = ph1.enter_context(tc.tile_pool(name="t_pool", bufs=5))
             w_pool = ph1.enter_context(tc.tile_pool(name="w_pool", bufs=2))
@@ -129,20 +136,35 @@ def tile_mixture_t_kernel(tc, inputs, biases, out):
             def turn_max(k):
                 xmt = ps_x.tile([P, SUB // 2, P], F32)
                 words = xm_of[k][:].bitcast(F32)
-                for n in range(BLOCKS[k][0] // 2):
+                nbs = (BLOCKS[k][0] - BLOCKS[k][1]) // 2
+                for n in range(nbs):
                     nc.tensor.transpose(xmt[:, n, :], words[:, n * P : (n + 1) * P], ident32[:])
+                for i in range(BLOCKS[k][1]):
+                    g = 2 * nbs + i
+                    nc.tensor.transpose(
+                        xmt[:, nbs, :].bitcast(BF16)[:, i * P : (i + 1) * P], xm_of[k][:, g * P : (g + 1) * P], ident[:]
+                    )
                 xmt_of[k] = xmt
 
             def reduce_max(k):
-                ng = BLOCKS[k][0]
+                ng, nf = BLOCKS[k]
+                nbg = ng - nf
                 g0 = g0_of[k]
                 nc.vector.tensor_reduce(
-                    out=nm32[:, g0 : g0 + ng].rearrange("q (n e) -> q n e", e=2),
-                    in_=xmt_of[k][:, 0 : ng // 2, :].bitcast(BF16).rearrange("q n (c e) -> q n e c", e=2),
+                    out=nm32[:, g0 : g0 + nbg].rearrange("q (n e) -> q n e", e=2),
+                    in_=xmt_of[k][:, 0 : nbg // 2, :].bitcast(BF16).rearrange("q n (c e) -> q n e c", e=2),
                     axis=AX.X,
                     op=ALU.max,
                     negate=True,
                 )
+                if nf > 0:
+                    nc.vector.tensor_reduce(
+                        out=nm32[:, g0 + nbg : g0 + ng],
+                        in_=xmt_of[k][:, nbg // 2, :].bitcast(BF16).rearrange("q (g c) -> q g c", g=nf),
+                        axis=AX.X,
+                        op=ALU.max,
+                        negate=True,
+                    )
                 nc.gpsimd.tensor_copy(out=nm16[:, g0 : g0 + ng], in_=nm32[:, g0 : g0 + ng])
 
             def forward(s):
@@ -224,25 +246,15 @@ def tile_mixture_t_kernel(tc, inputs, biases, out):
                     in_=grp_of[k][:, 0 : w * J],
                 )
 
-            warm_ps = ps_d.tile([P, 512], F32)
-
-            def warm(n):
-                nc.tensor.matmul(out=warm_ps[:, 0:n], lhsT=ones[:], rhs=warm_rhs[:, 0:n], start=True, stop=True)
-
             load(0)
             load(1)
             nc.sync.dma_start(out=b_raw[:], in_=bia)
             load(2)
             load(3)
 
-            for i in range(4):
-                warm(P)
-
             for s in range(-1, nu + 6):
                 if 0 <= s - 2 < nu:
                     backward(s - 2)
-                if 0 <= s < nu:
-                    warm(WARM_N)
                 if s + 1 < nu:
                     forward(s + 1)
                 if s == -1:

@@ -42,7 +42,7 @@ def tile_mixture_t_kernel(tc, inputs, biases, out):
         ng, nf = BLOCKS[k]
         nbg = ng - nf
         b_units = [("B", g, min(2, nbg - g)) for g in range(0, nbg, 2)]
-        f_units = [("F", nbg + f, 1) for f in range(nf)]
+        f_units = [("F", nbg + f, 2) for f in range(0, nf, 2)]
         mixed = []
         for i in range(max(len(b_units), len(f_units))):
             if i < len(b_units):
@@ -180,21 +180,28 @@ def tile_mixture_t_kernel(tc, inputs, biases, out):
                         )
                     fw_of[s] = xt
                 else:
-                    col = g0_of[k] + g
-                    df = ps_w.tile([P, J, P], F32, tag="fw")
-                    nc.tensor.matmul(
-                        out=df[:], lhsT=ident[:], rhs=t_of[k][:, :, g * P : (g + 1) * P], start=True, stop=False
-                    )
-                    for j in range(J):
+                    df0 = ps_w.tile([P, J, P], F32, tag="fw")
+                    df1 = ps_w.tile([P, J, P], F32, tag="fw")
+                    fw_of[s] = [df0, df1]
+                    for i in range(n):
                         nc.tensor.matmul(
-                            out=df[:, j, :],
-                            lhsT=nm32[:, col : col + 1].to_broadcast([P, P]),
-                            rhs=ident32[:],
-                            is_transpose=True,
-                            start=False,
-                            stop=(j == J - 1),
+                            out=fw_of[s][i][:],
+                            lhsT=ident[:],
+                            rhs=t_of[k][:, :, (g + i) * P : (g + i + 1) * P],
+                            start=True,
+                            stop=False,
                         )
-                    fw_of[s] = df
+                    for i in range(n):
+                        col = g0_of[k] + g + i
+                        for j in range(J):
+                            nc.tensor.matmul(
+                                out=fw_of[s][i][:, j, :],
+                                lhsT=nm32[:, col : col + 1].to_broadcast([P, P]),
+                                rhs=ident32[:],
+                                is_transpose=True,
+                                start=False,
+                                stop=(j == J - 1),
+                            )
 
             def exponent(s):
                 k, kind, g, n, i_in, n_in = units[s]
@@ -211,11 +218,12 @@ def tile_mixture_t_kernel(tc, inputs, biases, out):
                         )
                     esb_of[s] = e_sb
                 else:
-                    nc.scalar.activation(
-                        out=grp_of[k][:, g * 512 : (g + 1) * 512].rearrange("p (w j) -> p w j", j=J),
-                        in_=fw_of[s][:].rearrange("p j w -> p w j"),
-                        func=ACT.Exp,
-                    )
+                    for i in range(n):
+                        nc.scalar.activation(
+                            out=grp_of[k][:, (g + i) * 512 : (g + i + 1) * 512].rearrange("p (w j) -> p w j", j=J),
+                            in_=fw_of[s][i][:].rearrange("p j w -> p w j"),
+                            func=ACT.Exp,
+                        )
 
             def backward(s):
                 k, kind, g, n, i_in, n_in = units[s]

from contextlib import ExitStack

import concourse.mybir as mybir
from concourse.masks import make_identity

BF16 = mybir.dt.bfloat16
F32 = mybir.dt.float32
U32 = mybir.dt.uint32
U8 = mybir.dt.uint8
FP8X4 = mybir.dt.float8_e4m3fn_x4
ALU = mybir.AluOpType
ACT = mybir.ActivationFunctionType
AX = mybir.AxisListType

P = 128
B, C, HW, F = 4, 512, 4096, 256
J = 4
NPX = B * HW
NGRP = NPX // P
BLK = 1024
SUB = BLK // P
FLOPS = 2 * B * HW * C * F

S_EVERY = 3


def tile_mixture_t_kernel(tc, inputs, biases, out):
    nc = tc.nc
    BLOCKS = [(2, 0), (2, 0), (4, 0)] + [(8, 2)] * 12 + [(8, 0)] * 2 + [(4, 0), (4, 0)]
    OUT_BLOCKS = [8] * 15 + [4, 2, 2]
    x = inputs.rearrange("b (p j) h w -> b p j (h w)", j=J)
    bia = biases[0, 0].rearrange("(p j) f -> p j f", j=J)
    o = out.rearrange("b (t f) h w -> b t f (h w)", t=2)
    nb = len(BLOCKS)
    g0_of = [sum([b[0] for b in BLOCKS[:k]]) for k in range(nb)]
    assert g0_of[-1] + BLOCKS[-1][0] == NGRP and sum(OUT_BLOCKS) == NGRP

    units = []
    first_unit = []
    last_unit = []
    for k in range(nb):
        ng, nf = BLOCKS[k]
        nbg = ng - nf
        b_units = [("B", g, min(2, nbg - g)) for g in range(0, nbg, 2)]
        f_units = [("F", nbg + f, 2) for f in range(0, nf, 2)]
        mixed = []
        for i in range(max(len(b_units), len(f_units))):
            if i < len(b_units):
                mixed.append(b_units[i])
            if i < len(f_units):
                mixed.append(f_units[i])
        first_unit.append(len(units))
        for i in range(len(mixed)):
            units.append((k, mixed[i][0], mixed[i][1], mixed[i][2], i, len(mixed)))
        last_unit.append(len(units) - 1)
    nu = len(units)
    natural = []
    for k in range(nb):
        natural.extend([False] * (BLOCKS[k][0] - BLOCKS[k][1]) + [True] * BLOCKS[k][1])
    b_rank = {}
    for s in range(nu):
        if units[s][1] == "B":
            b_rank[s] = len(b_rank)

    with ExitStack() as ctx:
        ctx.enter_context(tc.manual_schedule())
        keep = ctx.enter_context(tc.tile_pool(name="keep", bufs=1))

        ident = keep.tile([P, P], BF16)
        ones = keep.tile([P, P], F32)
        codes = keep.tile([P, NPX], U32, align_bytes=64)
        scales = keep.tile([P, NPX], U8, align_bytes=64)
        ident32 = keep.tile([P, P], F32)
        nm16 = keep.tile([P, NGRP], BF16)
        nm32 = keep.tile([P, NGRP], F32)
        b_raw = keep.tile([P, J, F], BF16)
        sq = keep.tile([P, J, F], F32)
        js1 = keep.tile([P, 2, F], F32)
        js = keep.tile([P, F], F32)
        rs = keep.tile([P, F], F32)
        p_grp = keep.tile([P, F, J], BF16, align_bytes=64)
        p_codes = keep.tile([P, F], U32, align_bytes=64)
        p_scales = keep.tile([P, F], U8, align_bytes=64)

        make_identity(nc, ident[:])
        make_identity(nc, ident32[:])
        nc.gpsimd.memset(ones[:], 1.0)

        def bcast(g0, spans, mb_v):
            for n in range(spans):
                if natural[g0 + 2 * n]:
                    for i in range(2):
                        nc.tensor.transpose(
                            mb_v[:, n * P : (n + 1) * P].bitcast(BF16)[:, i * P : (i + 1) * P],
                            nm16[:, g0 + 2 * n + i : g0 + 2 * n + i + 1].to_broadcast([P, P]),
                            ident[:],
                        )
                else:
                    nc.tensor.transpose(
                        mb_v[:, n * P : (n + 1) * P],
                        nm16[:, g0 + 2 * n : g0 + 2 * n + 2].bitcast(F32).to_broadcast([P, P]),
                        ident32[:],
                    )

        with ExitStack() as ph1:
            ps_x = ph1.enter_context(tc.psum_pool(name="ps_x", bufs=1))
            ps_w = ph1.enter_context(tc.psum_pool(name="ps_w", bufs=4))
            ps_e = ph1.enter_context(tc.psum_pool(name="ps_e", bufs=3))
            t_pool = ph1.enter_context(tc.tile_pool(name="t_pool", bufs=5))
            w_pool = ph1.enter_context(tc.tile_pool(name="w_pool", bufs=2))
            e_pool = ph1.enter_context(tc.tile_pool(name="e_pool", bufs=3))
            g_pool = ph1.enter_context(tc.tile_pool(name="g_pool", bufs=4))
            t_of, a2_of, xm_of, xmt_of, fw_of, esb_of, eb_of, grp_of = {}, {}, {}, {}, {}, {}, {}, {}

            def load(k):
                t_in = t_pool.tile([P, J, BLK], BF16)
                w = BLOCKS[k][0] * P
                px = g0_of[k] * P
                nc.sync.dma_start(out=t_in[:, :, 0:w], in_=x[px // HW, :, :, px % HW : px % HW + w])
                t_of[k] = t_in

            def tree1(k):
                w = BLOCKS[k][0] * P
                a2 = w_pool.tile([P, 2, BLK], BF16)
                nc.vector.tensor_tensor(
                    out=a2[:, :, 0:w], in0=t_of[k][:, 0:2, 0:w], in1=t_of[k][:, 2:4, 0:w], op=ALU.max
                )
                a2_of[k] = a2

            def tree2(k):
                w = BLOCKS[k][0] * P
                xm = w_pool.tile([P, BLK], BF16)
                nc.vector.tensor_tensor(out=xm[:, 0:w], in0=a2_of[k][:, 0, 0:w], in1=a2_of[k][:, 1, 0:w], op=ALU.max)
                xm_of[k] = xm

            def turn_max(k):
                xmt = ps_x.tile([P, SUB // 2, P], F32)
                words = xm_of[k][:].bitcast(F32)
                nbs = (BLOCKS[k][0] - BLOCKS[k][1]) // 2
                for n in range(nbs):
                    nc.tensor.transpose(xmt[:, n, :], words[:, n * P : (n + 1) * P], ident32[:])
                for i in range(BLOCKS[k][1]):
                    g = 2 * nbs + i
                    nc.tensor.transpose(
                        xmt[:, nbs, :].bitcast(BF16)[:, i * P : (i + 1) * P], xm_of[k][:, g * P : (g + 1) * P], ident[:]
                    )
                xmt_of[k] = xmt

            def reduce_max(k):
                ng, nf = BLOCKS[k]
                nbg = ng - nf
                g0 = g0_of[k]
                nc.vector.tensor_reduce(
                    out=nm32[:, g0 : g0 + nbg].rearrange("q (n e) -> q n e", e=2),
                    in_=xmt_of[k][:, 0 : nbg // 2, :].bitcast(BF16).rearrange("q n (c e) -> q n e c", e=2),
                    axis=AX.X,
                    op=ALU.max,
                    negate=True,
                )
                if nf > 0:
                    nc.vector.tensor_reduce(
                        out=nm32[:, g0 + nbg : g0 + ng],
                        in_=xmt_of[k][:, nbg // 2, :].bitcast(BF16).rearrange("q (g c) -> q g c", g=nf),
                        axis=AX.X,
                        op=ALU.max,
                        negate=True,
                    )
                nc.gpsimd.tensor_copy(out=nm16[:, g0 : g0 + ng], in_=nm32[:, g0 : g0 + ng])

            def forward(s):
                k, kind, g, n, i_in, n_in = units[s]
                if i_in == 0:
                    grp = g_pool.tile([P, BLK * J], BF16, align_bytes=64)
                    grp_of[k] = grp
                if kind == "B":
                    xt = ps_w.tile([P, J, P], F32, tag="fw")
                    for j in range(J):
                        nc.tensor.transpose(
                            xt[:, j, :], t_of[k][:, j, g * P : (g + 2) * P].bitcast(F32), ident32[:]
                        )
                    fw_of[s] = xt
                else:
                    df0 = ps_w.tile([P, J, P], F32, tag="fw")
                    df1 = ps_w.tile([P, J, P], F32, tag="fw")
                    fw_of[s] = [df0, df1]
                    for i in range(n):
                        nc.tensor.matmul(
                            out=fw_of[s][i][:],
                            lhsT=ident[:],
                            rhs=t_of[k][:, :, (g + i) * P : (g + i + 1) * P],
                            start=True,
                            stop=False,
                        )
                    for i in range(n):
                        col = g0_of[k] + g + i
                        for j in range(J):
                            nc.tensor.matmul(
                                out=fw_of[s][i][:, j, :],
                                lhsT=nm32[:, col : col + 1].to_broadcast([P, P]),
                                rhs=ident32[:],
                                is_transpose=True,
                                start=False,
                                stop=(j == J - 1),
                            )

            def exponent(s):
                k, kind, g, n, i_in, n_in = units[s]
                if kind == "B":
                    e_sb = e_pool.tile([P, 2, C], BF16)
                    halves = fw_of[s][:].bitcast(BF16).rearrange("q (u t) (p e) -> q e u p t", t=2, e=2)
                    for i in range(n):
                        col = g0_of[k] + g + i
                        nc.scalar.activation(
                            out=e_sb[:, i, :].rearrange("q (u p t) -> q u p t", u=2, t=2),
                            in_=halves[:, i],
                            func=ACT.Exp,
                            bias=nm32[:, col : col + 1],
                        )
                    esb_of[s] = e_sb
                else:
                    for i in range(n):
                        nc.scalar.activation(
                            out=grp_of[k][:, (g + i) * 512 : (g + i + 1) * 512].rearrange("p (w j) -> p w j", j=J),
                            in_=fw_of[s][i][:].rearrange("p j w -> p w j"),
                            func=ACT.Exp,
                        )

            def backward(s):
                k, kind, g, n, i_in, n_in = units[s]
                if kind == "B":
                    eb = ps_e.tile([P, 2, 2, P], F32)
                    for i in range(n):
                        words = esb_of[s][:, i, :].bitcast(F32)
                        for u in range(2):
                            nc.tensor.transpose(eb[:, i, u, :], words[:, u * P : (u + 1) * P], ident32[:])
                    eb_of[s] = eb

            def copy_out(s):
                k, kind, g, n, i_in, n_in = units[s]
                if kind == "B":
                    dst = grp_of[k][:, g * 512 : (g + n) * 512].bitcast(F32).rearrange("p (q i u) -> p q i u", i=n, u=2)
                    src = eb_of[s][:, 0:n, :, :].rearrange("p i u q -> p q i u")
                    if b_rank[s] % S_EVERY == S_EVERY - 1:
                        nc.scalar.copy(out=dst, in_=src)
                    else:
                        nc.vector.tensor_copy(out=dst, in_=src)

            def quantise(k):
                c0 = g0_of[k] * P
                w = BLOCKS[k][0] * P
                nc.vector.quantize_mx(
                    out=codes[:, c0 : c0 + w].bitcast(FP8X4),
                    scales=scales[:, c0 : c0 + w],
                    in_=grp_of[k][:, 0 : w * J],
                )

            load(0)
            load(1)
            nc.sync.dma_start(out=b_raw[:], in_=bia)
            load(2)
            load(3)

            for s in range(-1, nu + 6):
                if 0 <= s - 2 < nu:
                    backward(s - 2)
                if s + 1 < nu:
                    forward(s + 1)
                if s == -1:
                    tree1(0)
                    tree2(0)
                    turn_max(0)
                    tree1(1)
                    tree2(1)
                    reduce_max(0)
                    turn_max(1)
                    reduce_max(1)
                if 0 <= s - 1 < nu:
                    exponent(s - 1)
                if 0 <= s - 3 < nu:
                    copy_out(s - 3)
                if 0 <= s < nu:
                    k, kind, g, n, i_in, n_in = units[s]
                    k2 = k + 2
                    if i_in == 0 and k + 4 < nb:
                        load(k + 4)
                    if k == 7 and i_in == 0:
                        nc.vector.reciprocal(out=rs[:], in_=col_sum[:, 0:F])
                        nc.gpsimd.tensor_tensor(
                            out=p_grp[:],
                            in0=sq[:].rearrange("p j f -> p f j"),
                            in1=rs[:].unsqueeze(2).to_broadcast([P, F, J]),
                            op=ALU.mult,
                        )
                    if 2 <= k + 1 < nb and i_in == min(1, n_in - 1):
                        reduce_max(k + 1)
                    if k2 < nb:
                        if i_in == 0:
                            tree1(k2)
                        if i_in == min(1, n_in - 1):
                            tree2(k2)
                        if i_in == n_in - 1:
                            turn_max(k2)
                    if k == 4 and i_in == 0:
                        nc.scalar.activation(out=sq[:], in_=b_raw[:], func=ACT.Square)
                        nc.gpsimd.tensor_tensor(out=js1[:], in0=sq[:, 0:2, :], in1=sq[:, 2:4, :], op=ALU.add)
                        nc.gpsimd.tensor_tensor(out=js[:], in0=js1[:, 0, :], in1=js1[:, 1, :], op=ALU.add)
                    if k == 6 and i_in == n_in - 1:
                        col_sum = ps_e.tile([P, 512], F32, tag="eb")
                        nc.tensor.matmul(out=col_sum[:, 0:F], lhsT=ones[:], rhs=js[:], start=True, stop=True)
                    if k == 9 and i_in == 1:
                        nc.vector.quantize_mx(
                            out=p_codes[:].bitcast(FP8X4),
                            scales=p_scales[:],
                            in_=p_grp[:].rearrange("p f j -> p (f j)"),
                        )
                for k in range(nb):
                    if last_unit[k] + 5 == s:
                        quantise(k)

        with ExitStack() as ph2:
            ps_m = ph2.enter_context(tc.psum_pool(name="ps_m", bufs=3))
            ps_s = ph2.enter_context(tc.psum_pool(name="ps_s", bufs=5))
            o_pool = ph2.enter_context(tc.tile_pool(name="o_pool", bufs=4))
            g0 = 0
            for ng in OUT_BLOCKS:
                w = ng * P
                px = g0 * P
                mb_v = ps_m.tile([P, BLK // 2], F32)
                bcast(g0, ng // 2, mb_v)
                for ft in range(2):
                    o_t = o_pool.tile([P, BLK], F32, tag="o%d" % ft)
                    for c0 in range(0, w, 512):
                        cw = min(512, w - c0)
                        cols = slice(px + c0, px + c0 + cw)
                        s_ps = ps_s.tile([P, 512], F32)
                        nc.tensor.matmul_mx(
                            out=s_ps[:, 0:cw],
                            lhsT=p_codes[:, ft * P : (ft + 1) * P].bitcast(FP8X4),
                            lhsT_scale=p_scales[:, ft * P : (ft + 1) * P],
                            rhs=codes[:, cols].bitcast(FP8X4),
                            rhs_scale=scales[:, cols],
                            start=True,
                            stop=True,
                        )
                        nc.scalar.activation(out=o_t[:, c0 : c0 + cw], in_=s_ps[:, 0:cw], func=ACT.Ln)
                    nc.vector.tensor_tensor(out=o_t[:, 0:w], in0=o_t[:, 0:w], in1=mb_v[:, 0 : w // 2].bitcast(BF16), op=ALU.subtract)
                    nc.sync.dma_start(out=o[px // HW, ft, :, px % HW : px % HW + w], in_=o_t[:, 0:w])
                g0 += ng
